import numpy as np
import ml_dtypes


def mxq(x, axis, fmt="e4m3"):
    dtype, down = {"e4m3": (ml_dtypes.float8_e4m3fn, 7), "e5m2": (ml_dtypes.float8_e5m2, 14)}[fmt]
    v = np.moveaxis(np.asarray(x, np.float32).astype(ml_dtypes.bfloat16).astype(np.float64), axis, -1)
    blocks = v.reshape(v.shape[:-1] + (-1, 32))
    amax = np.abs(blocks).max(-1, keepdims=True)
    byte = np.maximum(np.where(amax > 0, np.frexp(amax)[1] - 1 + 127, 0) - down, 1)
    scale = np.exp2(byte - 127.0)
    codes = (blocks / scale).astype(np.float32).astype(dtype).astype(np.float64)
    return np.moveaxis((codes * scale).reshape(v.shape), -1, axis)


WIDE = False


def mx_kscale(k):
    if not WIDE:
        return np.ones(k)
    levels = np.array([10, -10, 5, -5, 0])
    a = np.random.permutation(np.resize(levels, k // 512 * 4)).reshape(k // 512, 4)
    idx = np.arange(k)
    return np.exp2(a[idx // 512, idx % 128 // 32])


BF16 = ml_dtypes.bfloat16


def bf(x):
    return np.asarray(x, np.float32).astype(BF16)


def f64(x):
    return np.asarray(x).astype(np.float64)


B, S, D, H, HD = 1, 512, 128, 4, 128
I = H * HD


def silu(v):
    return v / (1.0 + np.exp(-v))


def setup_inputs():
    t = mx_kscale(I)
    h = silu(np.random.standard_normal((B, S, I))) * np.random.standard_normal((B, S, I))
    return {"h_inter": bf(h * t),
            "adjacency": bf(np.random.uniform(size=(B, H, S, S)) * 2.0 / np.sqrt(S)),
            "Wd": bf(np.random.standard_normal((I, D)) / np.sqrt(I) / t[:, None]),
            "eps": bf(np.random.standard_normal(H) * 0.2),
            "alpha": bf(1.0 + np.random.standard_normal(H) * 0.2)}


def reference(h_inter, adjacency, Wd, eps, alpha):
    h_heads = f64(h_inter).reshape(B, S, H, HD).transpose(0, 2, 1, 3)
    agg = mxq(f64(adjacency), 3, "e4m3") @ mxq(h_heads, 2, "e4m3")
    e = (1.0 + f64(eps))[None, :, None, None]
    a = f64(alpha)[None, :, None, None]
    h_gin = e * h_heads + a * agg
    h_comb = h_gin.transpose(0, 2, 1, 3).reshape(B, S, I)
    return mxq(h_comb, 2, "e4m3") @ mxq(f64(Wd), 0, "e4m3")

@@ -1,0 +1,189 @@
+from contextlib import ExitStack
+
+import concourse.mybir as mybir
+from concourse.masks import make_identity
+
+BF16 = mybir.dt.bfloat16
+F32 = mybir.dt.float32
+U32 = mybir.dt.uint32
+U8 = mybir.dt.uint8
+FP8X4 = mybir.dt.float8_e4m3fn_x4
+MULT = mybir.AluOpType.mult
+ADD = mybir.AluOpType.add
+COPY = mybir.ActivationFunctionType.Copy
+
+P = 128
+PACK = 4
+S = 512
+H = 4
+HD = 128
+D = 128
+RUN = 4
+
+FLOPS = 2 * H * S * S * HD + 2 * S * (H * HD) * D
+
+
+def regroup(engine_copy, grouped, rows):
+    engine_copy(
+        out=grouped.rearrange("p (x r) j -> p x j r", r=RUN),
+        in_=rows.rearrange("p j (x r) -> p x j r", r=RUN),
+    )
+
+
+def tile_llamamlp_halfwaygin_pa_s_kernel(tc, h_inter, adjacency, Wd, eps, alpha, out):
+    nc = tc.nc
+    with ExitStack() as ctx:
+        keep = ctx.enter_context(tc.tile_pool(name="keep", bufs=1))
+        stream = ctx.enter_context(tc.tile_pool(name="stream", bufs=2))
+        turned = ctx.enter_context(tc.psum_pool(name="turned", bufs=5))
+        sums = ctx.enter_context(tc.psum_pool(name="sums", bufs=2))
+        last = ctx.enter_context(tc.psum_pool(name="last", bufs=1))
+
+        h_sb = keep.tile([P, PACK, H * HD], BF16)
+        nc.sync.dma_start(
+            out=h_sb[:].rearrange("p (u e) i -> p u (e i)", u=2),
+            in_=h_inter[0].rearrange("(u p e) i -> p u (e i)", u=2, e=2),
+        )
+        a_sb = []
+        for n in range(H):
+            a_head = keep.tile([P, PACK, S], BF16, name="a_head%d" % n)
+            nc.sync.dma_start(
+                out=a_head[:].rearrange("p (u e) t -> p u (e t)", u=2),
+                in_=adjacency[0, n].rearrange("(u p e) t -> p u (e t)", u=2, e=2),
+            )
+            a_sb.append(a_head)
+        eps_bc = keep.tile([P, H], BF16)
+        nc.scalar.dma_start(out=eps_bc[:], in_=eps.partition_broadcast(P))
+        alpha_bc = keep.tile([P, H], BF16)
+        nc.scalar.dma_start(out=alpha_bc[:], in_=alpha.partition_broadcast(P))
+        wd_sb = keep.tile([P, PACK, D], BF16)
+        nc.scalar.dma_start(out=wd_sb[:], in_=Wd.rearrange("(n p) j -> p n j", n=H))
+
+        ident_bf = keep.tile([P, P], BF16)
+        make_identity(nc, ident_bf[:])
+        ident_f32 = keep.tile([P, P], F32)
+        make_identity(nc, ident_f32[:])
+
+        one_plus_eps = keep.tile([P, H], F32)
+        nc.vector.tensor_scalar_add(out=one_plus_eps[:], in0=eps_bc[:], scalar1=1.0)
+        alpha_f32 = keep.tile([P, H], F32)
+        nc.vector.tensor_copy(out=alpha_f32[:], in_=alpha_bc[:])
+
+        h_grouped = keep.tile([P, H * HD, PACK], BF16, align_bytes=64)
+        regroup(nc.vector.tensor_copy, h_grouped[:], h_sb[:])
+        h_codes = keep.tile([P, H * HD], U32, align_bytes=64)
+        h_scales = keep.tile([P, H * HD], U8, align_bytes=64)
+        nc.vector.quantize_mx(
+            out=h_codes[:].bitcast(FP8X4),
+            scales=h_scales[:],
+            in_=h_grouped[:].rearrange("p i c -> p (i c)"),
+        )
+
+        h_term = keep.tile([P, H, S], F32)
+        for n in range(H):
+            h_turned = turned.tile([P, 2 * PACK, P], BF16, tag="turned")
+            for c in range(PACK):
+                nc.tensor.transpose(h_turned[:, c, :], h_sb[:, c, n * HD : (n + 1) * HD], ident_bf[:])
+            nc.scalar.activation(
+                out=h_term[:, n, :],
+                in_=h_turned[:, 0:PACK, :].rearrange("p c s -> p (c s)"),
+                func=COPY,
+                scale=one_plus_eps[:, n : n + 1],
+            )
+
+        wd_grouped = keep.tile([P, D, PACK], BF16, align_bytes=64)
+        regroup(nc.vector.tensor_copy, wd_grouped[:], wd_sb[:])
+        wd_codes = keep.tile([P, D], U32, align_bytes=64)
+        wd_scales = keep.tile([P, D], U8, align_bytes=64)
+        nc.vector.quantize_mx(
+            out=wd_codes[:].bitcast(FP8X4),
+            scales=wd_scales[:],
+            in_=wd_grouped[:].rearrange("p j n -> p (j n)"),
+        )
+
+        a_grouped = {}
+        agg = {}
+        g_rows = keep.tile([P, H, S], BF16)
+
+        def turn_adjacency(n):
+            a_grouped[n] = stream.tile([P, S, PACK], BF16, align_bytes=64, name="a_grouped", tag="a_grouped")
+            words = (
+                a_grouped[n][:]
+                .rearrange("p s k -> p (s k)")
+                .bitcast(F32)
+                .rearrange("p (c s u) -> p c s u", c=PACK, u=2)
+            )
+            for half in range(2):
+                a_turned = turned.tile([P, 2, 2, P], F32, tag="turned")
+                for c in range(2):
+                    row_words = a_sb[n][:, 2 * half + c, :].bitcast(F32)
+                    for u in range(2):
+                        nc.tensor.transpose(a_turned[:, c, u, :], row_words[:, u * P : (u + 1) * P], ident_f32[:])
+                nc.scalar.copy(
+                    out=words[:, 2 * half : 2 * half + 2, :, :],
+                    in_=a_turned[:].rearrange("p c u s -> p c s u"),
+                )
+
+        def multiply(n):
+            a_codes = stream.tile([P, S], U32, align_bytes=64, tag="a_codes")
+            a_scales = stream.tile([P, S], U8, align_bytes=64, tag="a_scales")
+            nc.vector.quantize_mx(
+                out=a_codes[:].bitcast(FP8X4),
+                scales=a_scales[:],
+                in_=a_grouped[n][:].rearrange("p s k -> p (s k)"),
+            )
+            agg[n] = sums.tile([P, S], F32, name="agg", tag="agg")
+            nc.tensor.matmul_mx(
+                out=agg[n][:],
+                lhsT=h_codes[:, n * HD : (n + 1) * HD].bitcast(FP8X4),
+                lhsT_scale=h_scales[:, n * HD : (n + 1) * HD],
+                rhs=a_codes[:].bitcast(FP8X4),
+                rhs_scale=a_scales[:],
+                start=True,
+                stop=True,
+            )
+
+        def mix(n):
+            nc.vector.scalar_tensor_tensor(
+                out=g_rows[:, n, :],
+                in0=agg[n][:],
+                scalar=alpha_f32[:, n : n + 1],
+                in1=h_term[:, n, :],
+                op0=MULT,
+                op1=ADD,
+            )
+
+        for step in range(H + 2):
+            if step < H:
+                turn_adjacency(step)
+            if 1 <= step <= H:
+                multiply(step - 1)
+            if step >= 2:
+                mix(step - 2)
+
+        g_grouped = keep.tile([P, S, PACK], BF16, align_bytes=64)
+        regroup(nc.vector.tensor_copy, g_grouped[:], g_rows[:])
+        g_codes = keep.tile([P, S], U32, align_bytes=64)
+        g_scales = keep.tile([P, S], U8, align_bytes=64)
+        nc.vector.quantize_mx(
+            out=g_codes[:].bitcast(FP8X4),
+            scales=g_scales[:],
+            in_=g_grouped[:].rearrange("p s n -> p (s n)"),
+        )
+        out_ps = last.tile([P, PACK, D], F32)
+        for c in range(PACK):
+            nc.tensor.matmul_mx(
+                out=out_ps[:, c, :],
+                lhsT=g_codes[:, c * P : (c + 1) * P].bitcast(FP8X4),
+                lhsT_scale=g_scales[:, c * P : (c + 1) * P],
+                rhs=wd_codes[:].bitcast(FP8X4),
+                rhs_scale=wd_scales[:],
+                start=True,
+                stop=True,
+            )
+        out_sb = keep.tile([P, PACK, D], F32)
+        nc.scalar.copy(out=out_sb[:], in_=out_ps[:])
+        nc.sync.dma_start(
+            out=out[0].rearrange("(u p e) j -> p u (e j)", u=2, e=2),
+            in_=out_sb[:].rearrange("p (u e) j -> p u (e j)", u=2),
+        )

@@ -15,10 +15,13 @@ COPY = mybir.ActivationFunctionType.Copy
 P = 128
 PACK = 4
 S = 512
+HALF = S // 2
 H = 4
 HD = 128
 D = 128
 RUN = 4
+QUANTISE_LAG = 3
+MIX_LAG = 6
 
 FLOPS = 2 * H * S * S * HD + 2 * S * (H * HD) * D
 
@@ -34,28 +37,28 @@ def tile_llamamlp_halfwaygin_pa_s_kernel(tc, h_inter, adjacency, Wd, eps, alpha,
     nc = tc.nc
     with ExitStack() as ctx:
         keep = ctx.enter_context(tc.tile_pool(name="keep", bufs=1))
-        stream = ctx.enter_context(tc.tile_pool(name="stream", bufs=2))
-        turned = ctx.enter_context(tc.psum_pool(name="turned", bufs=5))
-        sums = ctx.enter_context(tc.psum_pool(name="sums", bufs=2))
-        last = ctx.enter_context(tc.psum_pool(name="last", bufs=1))
+        stream = ctx.enter_context(tc.tile_pool(name="stream", bufs=QUANTISE_LAG + 2))
+        turned = ctx.enter_context(tc.psum_pool(name="turned", bufs=4))
+        sums = ctx.enter_context(tc.psum_pool(name="sums", bufs=4))
+        ctx.enter_context(tc.manual_schedule())
 
+        eps_bc = keep.tile([P, H], BF16)
+        nc.scalar.dma_start(out=eps_bc[:], in_=eps.partition_broadcast(P))
+        alpha_bc = keep.tile([P, H], BF16)
+        nc.scalar.dma_start(out=alpha_bc[:], in_=alpha.partition_broadcast(P))
         h_sb = keep.tile([P, PACK, H * HD], BF16)
         nc.sync.dma_start(
             out=h_sb[:].rearrange("p (u e) i -> p u (e i)", u=2),
             in_=h_inter[0].rearrange("(u p e) i -> p u (e i)", u=2, e=2),
         )
-        a_sb = []
-        for n in range(H):
-            a_head = keep.tile([P, PACK, S], BF16, name="a_head%d" % n)
+        pieces = [(u, n) for u in range(2) for n in range(H)]
+        a_sb = {}
+        for u, n in pieces:
+            a_sb[u, n] = keep.tile([P, 2, S], BF16, name="a_sb_%d_%d" % (u, n))
             nc.sync.dma_start(
-                out=a_head[:].rearrange("p (u e) t -> p u (e t)", u=2),
-                in_=adjacency[0, n].rearrange("(u p e) t -> p u (e t)", u=2, e=2),
+                out=a_sb[u, n][:].rearrange("p e t -> p (e t)"),
+                in_=adjacency[0, n, u * HALF : (u + 1) * HALF, :].rearrange("(p e) t -> p (e t)", e=2),
             )
-            a_sb.append(a_head)
-        eps_bc = keep.tile([P, H], BF16)
-        nc.scalar.dma_start(out=eps_bc[:], in_=eps.partition_broadcast(P))
-        alpha_bc = keep.tile([P, H], BF16)
-        nc.scalar.dma_start(out=alpha_bc[:], in_=alpha.partition_broadcast(P))
         wd_sb = keep.tile([P, PACK, D], BF16)
         nc.scalar.dma_start(out=wd_sb[:], in_=Wd.rearrange("(n p) j -> p n j", n=H))
 
@@ -81,60 +84,53 @@ def tile_llamamlp_halfwaygin_pa_s_kernel(tc, h_inter, adjacency, Wd, eps, alpha,
 
         h_term = keep.tile([P, H, S], F32)
         for n in range(H):
-            h_turned = turned.tile([P, 2 * PACK, P], BF16, tag="turned")
+            h_turned = turned.tile([P, PACK, P], BF16, tag="turned")
             for c in range(PACK):
                 nc.tensor.transpose(h_turned[:, c, :], h_sb[:, c, n * HD : (n + 1) * HD], ident_bf[:])
-            nc.scalar.activation(
-                out=h_term[:, n, :],
-                in_=h_turned[:, 0:PACK, :].rearrange("p c s -> p (c s)"),
-                func=COPY,
-                scale=one_plus_eps[:, n : n + 1],
-            )
-
-        wd_grouped = keep.tile([P, D, PACK], BF16, align_bytes=64)
-        regroup(nc.vector.tensor_copy, wd_grouped[:], wd_sb[:])
-        wd_codes = keep.tile([P, D], U32, align_bytes=64)
-        wd_scales = keep.tile([P, D], U8, align_bytes=64)
-        nc.vector.quantize_mx(
-            out=wd_codes[:].bitcast(FP8X4),
-            scales=wd_scales[:],
-            in_=wd_grouped[:].rearrange("p j n -> p (j n)"),
-        )
+            if n < H - 1:
+                nc.scalar.activation(
+                    out=h_term[:, n, :],
+                    in_=h_turned[:].rearrange("p c s -> p (c s)"),
+                    func=COPY,
+                    scale=one_plus_eps[:, n : n + 1],
+                )
+            else:
+                nc.vector.tensor_scalar_mul(
+                    out=h_term[:, n, :],
+                    in0=h_turned[:].rearrange("p c s -> p (c s)"),
+                    scalar1=one_plus_eps[:, n : n + 1],
+                )
 
         a_grouped = {}
         agg = {}
         g_rows = keep.tile([P, H, S], BF16)
 
-        def turn_adjacency(n):
-            a_grouped[n] = stream.tile([P, S, PACK], BF16, align_bytes=64, name="a_grouped", tag="a_grouped")
-            words = (
-                a_grouped[n][:]
+        def turn_adjacency(u, n):
+            a_turned = turned.tile([P, 2, 2, P], F32, tag="turned")
+            for c in range(2):
+                row_words = a_sb[u, n][:, c, :].bitcast(F32)
+                for v in range(2):
+                    nc.tensor.transpose(a_turned[:, c, v, :], row_words[:, v * P : (v + 1) * P], ident_f32[:])
+            a_grouped[u, n] = stream.tile([P, HALF, PACK], BF16, align_bytes=64, name="a_grouped", tag="a_grouped")
+            nc.scalar.copy(
+                out=a_grouped[u, n][:]
                 .rearrange("p s k -> p (s k)")
                 .bitcast(F32)
-                .rearrange("p (c s u) -> p c s u", c=PACK, u=2)
+                .rearrange("p (c s v) -> p c s v", c=2, v=2),
+                in_=a_turned[:].rearrange("p c v s -> p c s v"),
             )
-            for half in range(2):
-                a_turned = turned.tile([P, 2, 2, P], F32, tag="turned")
-                for c in range(2):
-                    row_words = a_sb[n][:, 2 * half + c, :].bitcast(F32)
-                    for u in range(2):
-                        nc.tensor.transpose(a_turned[:, c, u, :], row_words[:, u * P : (u + 1) * P], ident_f32[:])
-                nc.scalar.copy(
-                    out=words[:, 2 * half : 2 * half + 2, :, :],
-                    in_=a_turned[:].rearrange("p c u s -> p c s u"),
-                )
 
-        def multiply(n):
-            a_codes = stream.tile([P, S], U32, align_bytes=64, tag="a_codes")
-            a_scales = stream.tile([P, S], U8, align_bytes=64, tag="a_scales")
+        def multiply(u, n):
+            a_codes = stream.tile([P, HALF], U32, align_bytes=64, tag="a_codes")
+            a_scales = stream.tile([P, HALF], U8, align_bytes=64, tag="a_scales")
             nc.vector.quantize_mx(
                 out=a_codes[:].bitcast(FP8X4),
                 scales=a_scales[:],
-                in_=a_grouped[n][:].rearrange("p s k -> p (s k)"),
+                in_=a_grouped[u, n][:].rearrange("p s k -> p (s k)"),
             )
-            agg[n] = sums.tile([P, S], F32, name="agg", tag="agg")
+            agg[u, n] = sums.tile([P, HALF], F32, name="agg", tag="sums")
             nc.tensor.matmul_mx(
-                out=agg[n][:],
+                out=agg[u, n][:],
                 lhsT=h_codes[:, n * HD : (n + 1) * HD].bitcast(FP8X4),
                 lhsT_scale=h_scales[:, n * HD : (n + 1) * HD],
                 rhs=a_codes[:].bitcast(FP8X4),
@@ -143,47 +139,64 @@ def tile_llamamlp_halfwaygin_pa_s_kernel(tc, h_inter, adjacency, Wd, eps, alpha,
                 stop=True,
             )
 
-        def mix(n):
+        def mix(u, n):
             nc.vector.scalar_tensor_tensor(
-                out=g_rows[:, n, :],
-                in0=agg[n][:],
+                out=g_rows[:, n, u * HALF : (u + 1) * HALF],
+                in0=agg[u, n][:],
                 scalar=alpha_f32[:, n : n + 1],
-                in1=h_term[:, n, :],
+                in1=h_term[:, n, u * HALF : (u + 1) * HALF],
                 op0=MULT,
                 op1=ADD,
             )
 
-        for step in range(H + 2):
-            if step < H:
-                turn_adjacency(step)
-            if 1 <= step <= H:
-                multiply(step - 1)
-            if step >= 2:
-                mix(step - 2)
+        wd_codes = keep.tile([P, D], U32, align_bytes=64)
+        wd_scales = keep.tile([P, D], U8, align_bytes=64)
 
-        g_grouped = keep.tile([P, S, PACK], BF16, align_bytes=64)
-        regroup(nc.vector.tensor_copy, g_grouped[:], g_rows[:])
-        g_codes = keep.tile([P, S], U32, align_bytes=64)
-        g_scales = keep.tile([P, S], U8, align_bytes=64)
-        nc.vector.quantize_mx(
-            out=g_codes[:].bitcast(FP8X4),
-            scales=g_scales[:],
-            in_=g_grouped[:].rearrange("p s n -> p (s n)"),
-        )
-        out_ps = last.tile([P, PACK, D], F32)
-        for c in range(PACK):
-            nc.tensor.matmul_mx(
-                out=out_ps[:, c, :],
-                lhsT=g_codes[:, c * P : (c + 1) * P].bitcast(FP8X4),
-                lhsT_scale=g_scales[:, c * P : (c + 1) * P],
-                rhs=wd_codes[:].bitcast(FP8X4),
-                rhs_scale=wd_scales[:],
-                start=True,
-                stop=True,
+        def quantise_wd():
+            wd_grouped = keep.tile([P, D, PACK], BF16, align_bytes=64)
+            regroup(nc.vector.tensor_copy, wd_grouped[:], wd_sb[:])
+            nc.vector.quantize_mx(
+                out=wd_codes[:].bitcast(FP8X4),
+                scales=wd_scales[:],
+                in_=wd_grouped[:].rearrange("p j n -> p (j n)"),
             )
-        out_sb = keep.tile([P, PACK, D], F32)
-        nc.scalar.copy(out=out_sb[:], in_=out_ps[:])
-        nc.sync.dma_start(
-            out=out[0].rearrange("(u p e) j -> p u (e j)", u=2, e=2),
-            in_=out_sb[:].rearrange("p (u e) j -> p u (e j)", u=2),
-        )
+
+        def project(u):
+            g_grouped = stream.tile([P, HALF, PACK], BF16, align_bytes=64, tag="g_grouped")
+            regroup(nc.vector.tensor_copy, g_grouped[:], g_rows[:, :, u * HALF : (u + 1) * HALF])
+            g_codes = stream.tile([P, HALF], U32, align_bytes=64, tag="g_codes")
+            g_scales = stream.tile([P, HALF], U8, align_bytes=64, tag="g_scales")
+            nc.vector.quantize_mx(
+                out=g_codes[:].bitcast(FP8X4),
+                scales=g_scales[:],
+                in_=g_grouped[:].rearrange("p s n -> p (s n)"),
+            )
+            out_ps = sums.tile([P, 2, D], F32, tag="sums")
+            for e in range(2):
+                nc.tensor.matmul_mx(
+                    out=out_ps[:, e, :],
+                    lhsT=g_codes[:, e * P : (e + 1) * P].bitcast(FP8X4),
+                    lhsT_scale=g_scales[:, e * P : (e + 1) * P],
+                    rhs=wd_codes[:].bitcast(FP8X4),
+                    rhs_scale=wd_scales[:],
+                    start=True,
+                    stop=True,
+                )
+            out_sb = stream.tile([P, 2, D], F32, tag="out_sb")
+            nc.scalar.copy(out=out_sb[:], in_=out_ps[:])
+            nc.sync.dma_start(
+                out=out[0, u * HALF : (u + 1) * HALF, :].rearrange("(p e) j -> p (e j)", e=2),
+                in_=out_sb[:].rearrange("p e j -> p (e j)"),
+            )
+
+        quantise_wd()
+        for step in range(len(pieces) + MIX_LAG):
+            if step < len(pieces):
+                turn_adjacency(*pieces[step])
+            if step >= MIX_LAG:
+                u, n = pieces[step - MIX_LAG]
+                mix(u, n)
+                if n == H - 1:
+                    project(u)
+            if QUANTISE_LAG <= step < len(pieces) + QUANTISE_LAG:
+                multiply(*pieces[step - QUANTISE_LAG])

@@ -15,13 +15,12 @@ COPY = mybir.ActivationFunctionType.Copy
 P = 128
 PACK = 4
 S = 512
-HALF = S // 2
 H = 4
 HD = 128
 D = 128
 RUN = 4
-QUANTISE_LAG = 3
-MIX_LAG = 6
+WARM_COLUMNS = 256
+WARM_PASSES = 8
 
 FLOPS = 2 * H * S * S * HD + 2 * S * (H * HD) * D
 
@@ -37,28 +36,45 @@ def tile_llamamlp_halfwaygin_pa_s_kernel(tc, h_inter, adjacency, Wd, eps, alpha,
     nc = tc.nc
     with ExitStack() as ctx:
         keep = ctx.enter_context(tc.tile_pool(name="keep", bufs=1))
-        stream = ctx.enter_context(tc.tile_pool(name="stream", bufs=QUANTISE_LAG + 2))
-        turned = ctx.enter_context(tc.psum_pool(name="turned", bufs=4))
-        sums = ctx.enter_context(tc.psum_pool(name="sums", bufs=4))
-        ctx.enter_context(tc.manual_schedule())
+        stream = ctx.enter_context(tc.tile_pool(name="stream", bufs=2))
+        turned = ctx.enter_context(tc.psum_pool(name="turned", bufs=5))
+        sums = ctx.enter_context(tc.psum_pool(name="sums", bufs=2))
+        last = ctx.enter_context(tc.psum_pool(name="last", bufs=1))
 
-        eps_bc = keep.tile([P, H], BF16)
-        nc.scalar.dma_start(out=eps_bc[:], in_=eps.partition_broadcast(P))
-        alpha_bc = keep.tile([P, H], BF16)
-        nc.scalar.dma_start(out=alpha_bc[:], in_=alpha.partition_broadcast(P))
+        ones = keep.tile([P, WARM_COLUMNS * PACK], BF16, align_bytes=64)
+        nc.vector.memset(ones[:], 1.0)
+        ones_codes = keep.tile([P, WARM_COLUMNS], U32, align_bytes=64)
+        ones_scales = keep.tile([P, WARM_COLUMNS], U8, align_bytes=64)
+        nc.vector.quantize_mx(out=ones_codes[:].bitcast(FP8X4), scales=ones_scales[:], in_=ones[:])
+        unread = last.tile([P, WARM_COLUMNS], F32, tag="out_ps")
+        for warm_pass in range(WARM_PASSES):
+            nc.tensor.matmul_mx(
+                out=unread[:],
+                lhsT=ones_codes[:, 0:P].bitcast(FP8X4),
+                lhsT_scale=ones_scales[:, 0:P],
+                rhs=ones_codes[:].bitcast(FP8X4),
+                rhs_scale=ones_scales[:],
+                start=True,
+                stop=True,
+            )
+
         h_sb = keep.tile([P, PACK, H * HD], BF16)
         nc.sync.dma_start(
             out=h_sb[:].rearrange("p (u e) i -> p u (e i)", u=2),
             in_=h_inter[0].rearrange("(u p e) i -> p u (e i)", u=2, e=2),
         )
-        pieces = [(u, n) for u in range(2) for n in range(H)]
-        a_sb = {}
-        for u, n in pieces:
-            a_sb[u, n] = keep.tile([P, 2, S], BF16, name="a_sb_%d_%d" % (u, n))
+        a_sb = []
+        for n in range(H):
+            a_head = keep.tile([P, PACK, S], BF16, name="a_head%d" % n)
             nc.sync.dma_start(
-                out=a_sb[u, n][:].rearrange("p e t -> p (e t)"),
-                in_=adjacency[0, n, u * HALF : (u + 1) * HALF, :].rearrange("(p e) t -> p (e t)", e=2),
+                out=a_head[:].rearrange("p (u e) t -> p u (e t)", u=2),
+                in_=adjacency[0, n].rearrange("(u p e) t -> p u (e t)", u=2, e=2),
             )
+            a_sb.append(a_head)
+        eps_bc = keep.tile([P, H], BF16)
+        nc.scalar.dma_start(out=eps_bc[:], in_=eps.partition_broadcast(P))
+        alpha_bc = keep.tile([P, H], BF16)
+        nc.scalar.dma_start(out=alpha_bc[:], in_=alpha.partition_broadcast(P))
         wd_sb = keep.tile([P, PACK, D], BF16)
         nc.scalar.dma_start(out=wd_sb[:], in_=Wd.rearrange("(n p) j -> p n j", n=H))
 
@@ -84,53 +100,60 @@ def tile_llamamlp_halfwaygin_pa_s_kernel(tc, h_inter, adjacency, Wd, eps, alpha,
 
         h_term = keep.tile([P, H, S], F32)
         for n in range(H):
-            h_turned = turned.tile([P, PACK, P], BF16, tag="turned")
+            h_turned = turned.tile([P, 2 * PACK, P], BF16, tag="turned")
             for c in range(PACK):
                 nc.tensor.transpose(h_turned[:, c, :], h_sb[:, c, n * HD : (n + 1) * HD], ident_bf[:])
-            if n < H - 1:
-                nc.scalar.activation(
-                    out=h_term[:, n, :],
-                    in_=h_turned[:].rearrange("p c s -> p (c s)"),
-                    func=COPY,
-                    scale=one_plus_eps[:, n : n + 1],
-                )
-            else:
-                nc.vector.tensor_scalar_mul(
-                    out=h_term[:, n, :],
-                    in0=h_turned[:].rearrange("p c s -> p (c s)"),
-                    scalar1=one_plus_eps[:, n : n + 1],
-                )
+            nc.scalar.activation(
+                out=h_term[:, n, :],
+                in_=h_turned[:, 0:PACK, :].rearrange("p c s -> p (c s)"),
+                func=COPY,
+                scale=one_plus_eps[:, n : n + 1],
+            )
+
+        wd_grouped = keep.tile([P, D, PACK], BF16, align_bytes=64)
+        regroup(nc.vector.tensor_copy, wd_grouped[:], wd_sb[:])
+        wd_codes = keep.tile([P, D], U32, align_bytes=64)
+        wd_scales = keep.tile([P, D], U8, align_bytes=64)
+        nc.vector.quantize_mx(
+            out=wd_codes[:].bitcast(FP8X4),
+            scales=wd_scales[:],
+            in_=wd_grouped[:].rearrange("p j n -> p (j n)"),
+        )
 
         a_grouped = {}
         agg = {}
         g_rows = keep.tile([P, H, S], BF16)
 
-        def turn_adjacency(u, n):
-            a_turned = turned.tile([P, 2, 2, P], F32, tag="turned")
-            for c in range(2):
-                row_words = a_sb[u, n][:, c, :].bitcast(F32)
-                for v in range(2):
-                    nc.tensor.transpose(a_turned[:, c, v, :], row_words[:, v * P : (v + 1) * P], ident_f32[:])
-            a_grouped[u, n] = stream.tile([P, HALF, PACK], BF16, align_bytes=64, name="a_grouped", tag="a_grouped")
-            nc.scalar.copy(
-                out=a_grouped[u, n][:]
+        def turn_adjacency(n):
+            a_grouped[n] = stream.tile([P, S, PACK], BF16, align_bytes=64, name="a_grouped", tag="a_grouped")
+            words = (
+                a_grouped[n][:]
                 .rearrange("p s k -> p (s k)")
                 .bitcast(F32)
-                .rearrange("p (c s v) -> p c s v", c=2, v=2),
-                in_=a_turned[:].rearrange("p c v s -> p c s v"),
+                .rearrange("p (c s u) -> p c s u", c=PACK, u=2)
             )
+            for half in range(2):
+                a_turned = turned.tile([P, 2, 2, P], F32, tag="turned")
+                for c in range(2):
+                    row_words = a_sb[n][:, 2 * half + c, :].bitcast(F32)
+                    for u in range(2):
+                        nc.tensor.transpose(a_turned[:, c, u, :], row_words[:, u * P : (u + 1) * P], ident_f32[:])
+                nc.scalar.copy(
+                    out=words[:, 2 * half : 2 * half + 2, :, :],
+                    in_=a_turned[:].rearrange("p c u s -> p c s u"),
+                )
 
-        def multiply(u, n):
-            a_codes = stream.tile([P, HALF], U32, align_bytes=64, tag="a_codes")
-            a_scales = stream.tile([P, HALF], U8, align_bytes=64, tag="a_scales")
+        def multiply(n):
+            a_codes = stream.tile([P, S], U32, align_bytes=64, tag="a_codes")
+            a_scales = stream.tile([P, S], U8, align_bytes=64, tag="a_scales")
             nc.vector.quantize_mx(
                 out=a_codes[:].bitcast(FP8X4),
                 scales=a_scales[:],
-                in_=a_grouped[u, n][:].rearrange("p s k -> p (s k)"),
+                in_=a_grouped[n][:].rearrange("p s k -> p (s k)"),
             )
-            agg[u, n] = sums.tile([P, HALF], F32, name="agg", tag="sums")
+            agg[n] = sums.tile([P, S], F32, name="agg", tag="agg")
             nc.tensor.matmul_mx(
-                out=agg[u, n][:],
+                out=agg[n][:],
                 lhsT=h_codes[:, n * HD : (n + 1) * HD].bitcast(FP8X4),
                 lhsT_scale=h_scales[:, n * HD : (n + 1) * HD],
                 rhs=a_codes[:].bitcast(FP8X4),
@@ -139,64 +162,47 @@ def tile_llamamlp_halfwaygin_pa_s_kernel(tc, h_inter, adjacency, Wd, eps, alpha,
                 stop=True,
             )
 
-        def mix(u, n):
+        def mix(n):
             nc.vector.scalar_tensor_tensor(
-                out=g_rows[:, n, u * HALF : (u + 1) * HALF],
-                in0=agg[u, n][:],
+                out=g_rows[:, n, :],
+                in0=agg[n][:],
                 scalar=alpha_f32[:, n : n + 1],
-                in1=h_term[:, n, u * HALF : (u + 1) * HALF],
+                in1=h_term[:, n, :],
                 op0=MULT,
                 op1=ADD,
             )
 
-        wd_codes = keep.tile([P, D], U32, align_bytes=64)
-        wd_scales = keep.tile([P, D], U8, align_bytes=64)
+        for step in range(H + 2):
+            if step < H:
+                turn_adjacency(step)
+            if 1 <= step <= H:
+                multiply(step - 1)
+            if step >= 2:
+                mix(step - 2)
 
-        def quantise_wd():
-            wd_grouped = keep.tile([P, D, PACK], BF16, align_bytes=64)
-            regroup(nc.vector.tensor_copy, wd_grouped[:], wd_sb[:])
-            nc.vector.quantize_mx(
-                out=wd_codes[:].bitcast(FP8X4),
-                scales=wd_scales[:],
-                in_=wd_grouped[:].rearrange("p j n -> p (j n)"),
+        g_grouped = keep.tile([P, S, PACK], BF16, align_bytes=64)
+        regroup(nc.vector.tensor_copy, g_grouped[:], g_rows[:])
+        g_codes = keep.tile([P, S], U32, align_bytes=64)
+        g_scales = keep.tile([P, S], U8, align_bytes=64)
+        nc.vector.quantize_mx(
+            out=g_codes[:].bitcast(FP8X4),
+            scales=g_scales[:],
+            in_=g_grouped[:].rearrange("p s n -> p (s n)"),
+        )
+        out_ps = last.tile([P, PACK, D], F32, tag="out_ps")
+        for c in range(PACK):
+            nc.tensor.matmul_mx(
+                out=out_ps[:, c, :],
+                lhsT=g_codes[:, c * P : (c + 1) * P].bitcast(FP8X4),
+                lhsT_scale=g_scales[:, c * P : (c + 1) * P],
+                rhs=wd_codes[:].bitcast(FP8X4),
+                rhs_scale=wd_scales[:],
+                start=True,
+                stop=True,
             )
-
-        def project(u):
-            g_grouped = stream.tile([P, HALF, PACK], BF16, align_bytes=64, tag="g_grouped")
-            regroup(nc.vector.tensor_copy, g_grouped[:], g_rows[:, :, u * HALF : (u + 1) * HALF])
-            g_codes = stream.tile([P, HALF], U32, align_bytes=64, tag="g_codes")
-            g_scales = stream.tile([P, HALF], U8, align_bytes=64, tag="g_scales")
-            nc.vector.quantize_mx(
-                out=g_codes[:].bitcast(FP8X4),
-                scales=g_scales[:],
-                in_=g_grouped[:].rearrange("p s n -> p (s n)"),
-            )
-            out_ps = sums.tile([P, 2, D], F32, tag="sums")
-            for e in range(2):
-                nc.tensor.matmul_mx(
-                    out=out_ps[:, e, :],
-                    lhsT=g_codes[:, e * P : (e + 1) * P].bitcast(FP8X4),
-                    lhsT_scale=g_scales[:, e * P : (e + 1) * P],
-                    rhs=wd_codes[:].bitcast(FP8X4),
-                    rhs_scale=wd_scales[:],
-                    start=True,
-                    stop=True,
-                )
-            out_sb = stream.tile([P, 2, D], F32, tag="out_sb")
-            nc.scalar.copy(out=out_sb[:], in_=out_ps[:])
-            nc.sync.dma_start(
-                out=out[0, u * HALF : (u + 1) * HALF, :].rearrange("(p e) j -> p (e j)", e=2),
-                in_=out_sb[:].rearrange("p e j -> p (e j)"),
-            )
-
-        quantise_wd()
-        for step in range(len(pieces) + MIX_LAG):
-            if step < len(pieces):
-                turn_adjacency(*pieces[step])
-            if step >= MIX_LAG:
-                u, n = pieces[step - MIX_LAG]
-                mix(u, n)
-                if n == H - 1:
-                    project(u)
-            if QUANTISE_LAG <= step < len(pieces) + QUANTISE_LAG:
-                multiply(*pieces[step - QUANTISE_LAG])
+        out_sb = keep.tile([P, PACK, D], F32)
+        nc.scalar.copy(out=out_sb[:], in_=out_ps[:])
+        nc.sync.dma_start(
+            out=out[0].rearrange("(u p e) j -> p u (e j)", u=2, e=2),
+            in_=out_sb[:].rearrange("p (u e) j -> p u (e j)", u=2),
+        )

@@ -18,6 +18,14 @@ S = 512
 H = 4
 HD = 128
 D = 128
+C = 4
+PIECES = 2 * C
+QUANTISE_LAG = 2
+MULTIPLY_LAG = 3
+MIX_LAG = 4
+G_TURN_LAG = 7
+G_QUANTISE_LAG = 9
+OUT_LAG = 10
 RUN = 4
 WARM_COLUMNS = 256
 WARM_PASSES = 8
@@ -36,10 +44,40 @@ def tile_llamamlp_halfwaygin_pa_s_kernel(tc, h_inter, adjacency, Wd, eps, alpha,
     nc = tc.nc
     with ExitStack() as ctx:
         keep = ctx.enter_context(tc.tile_pool(name="keep", bufs=1))
-        stream = ctx.enter_context(tc.tile_pool(name="stream", bufs=2))
-        turned = ctx.enter_context(tc.psum_pool(name="turned", bufs=5))
-        sums = ctx.enter_context(tc.psum_pool(name="sums", bufs=2))
+        turned = ctx.enter_context(tc.psum_pool(name="turned", bufs=4))
+        sums = ctx.enter_context(tc.psum_pool(name="sums", bufs=3))
         last = ctx.enter_context(tc.psum_pool(name="last", bufs=1))
+        ctx.enter_context(tc.manual_schedule())
+
+        eps_bc = keep.tile([P, H], BF16)
+        nc.scalar.dma_start(out=eps_bc[:], in_=eps.partition_broadcast(P))
+        alpha_bc = keep.tile([P, H], BF16)
+        nc.scalar.dma_start(out=alpha_bc[:], in_=alpha.partition_broadcast(P))
+        wd_sb = keep.tile([P, PACK, D], BF16)
+        nc.sync.dma_start(
+            out=wd_sb[:].rearrange("p (u e) j -> p u (e j)", u=2),
+            in_=Wd.rearrange("(u p e) j -> p u (e j)", u=2, e=2),
+        )
+        h_sb = keep.tile([P, C, H * HD], BF16)
+        nc.sync.dma_start(
+            out=h_sb[:].rearrange("p (u e) i -> p u (e i)", u=2),
+            in_=h_inter[0].rearrange("(u p e) i -> p u (e i)", u=2, e=2),
+        )
+        a_rows = adjacency[0].rearrange("n (u p e) t -> u e p n t", u=2, e=2)
+        a_sb = []
+        for x in range(PIECES):
+            c, pair = divmod(x, 2)
+            a_piece = keep.tile([P, 2, S], BF16, name="a_piece%d" % x)
+            nc.sync.dma_start(out=a_piece[:], in_=a_rows[c // 2, c % 2][:, 2 * pair : 2 * pair + 2, :])
+            a_sb.append(a_piece)
+
+        zero = keep.tile([P, 1], F32)
+        nc.vector.memset(zero[:], 0.0)
+        unread_column = keep.tile([P, 1], F32)
+        nc.scalar.activation(out=unread_column[:], in_=zero[:], func=COPY)
+
+        ident = keep.tile([P, P], F32)
+        make_identity(nc, ident[:])
 
         ones = keep.tile([P, WARM_COLUMNS * PACK], BF16, align_bytes=64)
         nc.vector.memset(ones[:], 1.0)
@@ -58,151 +96,155 @@ def tile_llamamlp_halfwaygin_pa_s_kernel(tc, h_inter, adjacency, Wd, eps, alpha,
                 stop=True,
             )
 
-        h_sb = keep.tile([P, PACK, H * HD], BF16)
-        nc.sync.dma_start(
-            out=h_sb[:].rearrange("p (u e) i -> p u (e i)", u=2),
-            in_=h_inter[0].rearrange("(u p e) i -> p u (e i)", u=2, e=2),
-        )
-        a_sb = []
-        for n in range(H):
-            a_head = keep.tile([P, PACK, S], BF16, name="a_head%d" % n)
-            nc.sync.dma_start(
-                out=a_head[:].rearrange("p (u e) t -> p u (e t)", u=2),
-                in_=adjacency[0, n].rearrange("(u p e) t -> p u (e t)", u=2, e=2),
-            )
-            a_sb.append(a_head)
-        eps_bc = keep.tile([P, H], BF16)
-        nc.scalar.dma_start(out=eps_bc[:], in_=eps.partition_broadcast(P))
-        alpha_bc = keep.tile([P, H], BF16)
-        nc.scalar.dma_start(out=alpha_bc[:], in_=alpha.partition_broadcast(P))
-        wd_sb = keep.tile([P, PACK, D], BF16)
-        nc.scalar.dma_start(out=wd_sb[:], in_=Wd.rearrange("(n p) j -> p n j", n=H))
-
-        ident_bf = keep.tile([P, P], BF16)
-        make_identity(nc, ident_bf[:])
-        ident_f32 = keep.tile([P, P], F32)
-        make_identity(nc, ident_f32[:])
+        wd_grouped = keep.tile([P, D, PACK], BF16, align_bytes=64)
+        wd_codes = keep.tile([P, D], U32, align_bytes=64)
+        wd_scales = keep.tile([P, D], U8, align_bytes=64)
+        regroup(nc.vector.tensor_copy, wd_grouped[:], wd_sb[:])
 
         one_plus_eps = keep.tile([P, H], F32)
         nc.vector.tensor_scalar_add(out=one_plus_eps[:], in0=eps_bc[:], scalar1=1.0)
         alpha_f32 = keep.tile([P, H], F32)
         nc.vector.tensor_copy(out=alpha_f32[:], in_=alpha_bc[:])
 
+        nc.vector.quantize_mx(
+            out=wd_codes[:].bitcast(FP8X4),
+            scales=wd_scales[:],
+            in_=wd_grouped[:].rearrange("p j k -> p (j k)"),
+        )
+
         h_grouped = keep.tile([P, H * HD, PACK], BF16, align_bytes=64)
-        regroup(nc.vector.tensor_copy, h_grouped[:], h_sb[:])
         h_codes = keep.tile([P, H * HD], U32, align_bytes=64)
         h_scales = keep.tile([P, H * HD], U8, align_bytes=64)
+        regroup(nc.vector.tensor_copy, h_grouped[:], h_sb[:])
         nc.vector.quantize_mx(
             out=h_codes[:].bitcast(FP8X4),
             scales=h_scales[:],
             in_=h_grouped[:].rearrange("p i c -> p (i c)"),
         )
 
-        h_term = keep.tile([P, H, S], F32)
+        h_term = keep.tile([P, C, H * HD], F32)
         for n in range(H):
-            h_turned = turned.tile([P, 2 * PACK, P], BF16, tag="turned")
-            for c in range(PACK):
-                nc.tensor.transpose(h_turned[:, c, :], h_sb[:, c, n * HD : (n + 1) * HD], ident_bf[:])
-            nc.scalar.activation(
-                out=h_term[:, n, :],
-                in_=h_turned[:, 0:PACK, :].rearrange("p c s -> p (c s)"),
-                func=COPY,
-                scale=one_plus_eps[:, n : n + 1],
-            )
-
-        wd_grouped = keep.tile([P, D, PACK], BF16, align_bytes=64)
-        regroup(nc.vector.tensor_copy, wd_grouped[:], wd_sb[:])
-        wd_codes = keep.tile([P, D], U32, align_bytes=64)
-        wd_scales = keep.tile([P, D], U8, align_bytes=64)
-        nc.vector.quantize_mx(
-            out=wd_codes[:].bitcast(FP8X4),
-            scales=wd_scales[:],
-            in_=wd_grouped[:].rearrange("p j n -> p (j n)"),
-        )
-
-        a_grouped = {}
-        agg = {}
-        g_rows = keep.tile([P, H, S], BF16)
-
-        def turn_adjacency(n):
-            a_grouped[n] = stream.tile([P, S, PACK], BF16, align_bytes=64, name="a_grouped", tag="a_grouped")
-            words = (
-                a_grouped[n][:]
-                .rearrange("p s k -> p (s k)")
-                .bitcast(F32)
-                .rearrange("p (c s u) -> p c s u", c=PACK, u=2)
-            )
-            for half in range(2):
-                a_turned = turned.tile([P, 2, 2, P], F32, tag="turned")
-                for c in range(2):
-                    row_words = a_sb[n][:, 2 * half + c, :].bitcast(F32)
-                    for u in range(2):
-                        nc.tensor.transpose(a_turned[:, c, u, :], row_words[:, u * P : (u + 1) * P], ident_f32[:])
-                nc.scalar.copy(
-                    out=words[:, 2 * half : 2 * half + 2, :, :],
-                    in_=a_turned[:].rearrange("p c u s -> p c s u"),
+            cols = slice(n * HD, (n + 1) * HD)
+            if n < H - 1:
+                nc.scalar.activation(
+                    out=h_term[:, :, cols], in_=h_sb[:, :, cols], func=COPY, scale=one_plus_eps[:, n : n + 1]
+                )
+            else:
+                nc.vector.tensor_scalar_mul(
+                    out=h_term[:, :, cols], in0=h_sb[:, :, cols], scalar1=one_plus_eps[:, n : n + 1]
                 )
 
-        def multiply(n):
-            a_codes = stream.tile([P, S], U32, align_bytes=64, tag="a_codes")
-            a_scales = stream.tile([P, S], U8, align_bytes=64, tag="a_scales")
+        a_grouped = {}
+        a_codes = {}
+        a_scales = {}
+        agg = {}
+        g_sb = [keep.tile([P, H * HD], BF16, align_bytes=64, name="g_sb%d" % c) for c in range(C)]
+
+        def turn_adjacency(x):
+            a_turned = turned.tile([P, 2, 2, P], F32, tag="turned")
+            for i in range(2):
+                row_words = a_sb[x][:, i, :].bitcast(F32)
+                for u in range(2):
+                    nc.tensor.transpose(a_turned[:, i, u, :], row_words[:, u * P : (u + 1) * P], ident[:])
+            a_grouped[x] = keep.tile([P, 2, P, PACK], BF16, align_bytes=64, name="a_grouped%d" % x)
+            nc.scalar.copy(
+                out=a_grouped[x][:]
+                .rearrange("p i s k -> p (i s k)")
+                .bitcast(F32)
+                .rearrange("p (i s u) -> p i s u", i=2, u=2),
+                in_=a_turned[:].rearrange("p i u s -> p i s u"),
+            )
+
+        def quantise_adjacency(x):
+            a_codes[x] = keep.tile([P, 2 * P], U32, align_bytes=64, name="a_codes%d" % x)
+            a_scales[x] = keep.tile([P, 2 * P], U8, align_bytes=64, name="a_scales%d" % x)
             nc.vector.quantize_mx(
-                out=a_codes[:].bitcast(FP8X4),
-                scales=a_scales[:],
-                in_=a_grouped[n][:].rearrange("p s k -> p (s k)"),
+                out=a_codes[x][:].bitcast(FP8X4),
+                scales=a_scales[x][:],
+                in_=a_grouped[x][:].rearrange("p i s k -> p (i s k)"),
             )
-            agg[n] = sums.tile([P, S], F32, name="agg", tag="agg")
+
+        def multiply(x):
+            agg[x] = sums.tile([P, 2, HD], F32, name="agg", tag="agg")
+            for i in range(2):
+                n = 2 * (x % 2) + i
+                nc.tensor.matmul_mx(
+                    out=agg[x][:, i, :],
+                    lhsT=a_codes[x][:, i * P : (i + 1) * P].bitcast(FP8X4),
+                    lhsT_scale=a_scales[x][:, i * P : (i + 1) * P],
+                    rhs=h_codes[:, n * HD : (n + 1) * HD].bitcast(FP8X4),
+                    rhs_scale=h_scales[:, n * HD : (n + 1) * HD],
+                    start=True,
+                    stop=True,
+                )
+
+        def mix(x):
+            c, pair = divmod(x, 2)
+            for i in range(2):
+                n = 2 * pair + i
+                cols = slice(n * HD, (n + 1) * HD)
+                nc.vector.scalar_tensor_tensor(
+                    out=g_sb[c][:, cols],
+                    in0=agg[x][:, i, :],
+                    scalar=alpha_f32[:, n : n + 1],
+                    in1=h_term[:, c, cols],
+                    op0=MULT,
+                    op1=ADD,
+                )
+
+        g_grouped = {}
+        g_codes = {}
+        g_scales = {}
+        out_sb = keep.tile([P, C, D], F32)
+        out_rows = out[0].rearrange("(u p e) j -> u e p j", u=2, e=2)
+
+        def turn_g(c):
+            g_turned = turned.tile([P, 2, P], F32, tag="turned")
+            row_words = g_sb[c][:].bitcast(F32)
+            for u in range(2):
+                nc.tensor.transpose(g_turned[:, u, :], row_words[:, u * P : (u + 1) * P], ident[:])
+            g_grouped[c] = keep.tile([P, P, PACK], BF16, align_bytes=64, name="g_grouped%d" % c)
+            nc.scalar.copy(
+                out=g_grouped[c][:].rearrange("p s k -> p (s k)").bitcast(F32).rearrange("p (s u) -> p s u", u=2),
+                in_=g_turned[:].rearrange("p u s -> p s u"),
+            )
+
+        def quantise_g(c):
+            g_codes[c] = keep.tile([P, P], U32, align_bytes=64, name="g_codes%d" % c)
+            g_scales[c] = keep.tile([P, P], U8, align_bytes=64, name="g_scales%d" % c)
+            nc.vector.quantize_mx(
+                out=g_codes[c][:].bitcast(FP8X4),
+                scales=g_scales[c][:],
+                in_=g_grouped[c][:].rearrange("p s k -> p (s k)"),
+            )
+
+        def project(c):
+            out_ps = last.tile([P, D], F32, tag="out_ps")
             nc.tensor.matmul_mx(
-                out=agg[n][:],
-                lhsT=h_codes[:, n * HD : (n + 1) * HD].bitcast(FP8X4),
-                lhsT_scale=h_scales[:, n * HD : (n + 1) * HD],
-                rhs=a_codes[:].bitcast(FP8X4),
-                rhs_scale=a_scales[:],
-                start=True,
-                stop=True,
-            )
-
-        def mix(n):
-            nc.vector.scalar_tensor_tensor(
-                out=g_rows[:, n, :],
-                in0=agg[n][:],
-                scalar=alpha_f32[:, n : n + 1],
-                in1=h_term[:, n, :],
-                op0=MULT,
-                op1=ADD,
-            )
-
-        for step in range(H + 2):
-            if step < H:
-                turn_adjacency(step)
-            if 1 <= step <= H:
-                multiply(step - 1)
-            if step >= 2:
-                mix(step - 2)
-
-        g_grouped = keep.tile([P, S, PACK], BF16, align_bytes=64)
-        regroup(nc.vector.tensor_copy, g_grouped[:], g_rows[:])
-        g_codes = keep.tile([P, S], U32, align_bytes=64)
-        g_scales = keep.tile([P, S], U8, align_bytes=64)
-        nc.vector.quantize_mx(
-            out=g_codes[:].bitcast(FP8X4),
-            scales=g_scales[:],
-            in_=g_grouped[:].rearrange("p s n -> p (s n)"),
-        )
-        out_ps = last.tile([P, PACK, D], F32, tag="out_ps")
-        for c in range(PACK):
-            nc.tensor.matmul_mx(
-                out=out_ps[:, c, :],
-                lhsT=g_codes[:, c * P : (c + 1) * P].bitcast(FP8X4),
-                lhsT_scale=g_scales[:, c * P : (c + 1) * P],
+                out=out_ps[:],
+                lhsT=g_codes[c][:].bitcast(FP8X4),
+                lhsT_scale=g_scales[c][:],
                 rhs=wd_codes[:].bitcast(FP8X4),
                 rhs_scale=wd_scales[:],
                 start=True,
                 stop=True,
             )
-        out_sb = keep.tile([P, PACK, D], F32)
-        nc.scalar.copy(out=out_sb[:], in_=out_ps[:])
-        nc.sync.dma_start(
-            out=out[0].rearrange("(u p e) j -> p u (e j)", u=2, e=2),
-            in_=out_sb[:].rearrange("p (u e) j -> p u (e j)", u=2),
-        )
+            nc.scalar.copy(out=out_sb[:, c, :], in_=out_ps[:])
+            nc.sync.dma_start(out=out_rows[c // 2, c % 2], in_=out_sb[:, c, :])
+
+        def per_piece(stage, x):
+            if 0 <= x < PIECES:
+                stage(x)
+
+        def per_slice(stage, twice_c):
+            if twice_c % 2 == 0 and 0 <= twice_c < PIECES:
+                stage(twice_c // 2)
+
+        for step in range(PIECES + OUT_LAG):
+            per_piece(turn_adjacency, step)
+            per_piece(multiply, step - MULTIPLY_LAG)
+            per_piece(quantise_adjacency, step - QUANTISE_LAG)
+            per_slice(quantise_g, step - G_QUANTISE_LAG)
+            per_slice(project, step - OUT_LAG)
+            per_piece(mix, step - MIX_LAG)
+            per_slice(turn_g, step - G_TURN_LAG)

@@ -45,8 +45,9 @@ def tile_llamamlp_halfwaygin_pa_s_kernel(tc, h_inter, adjacency, Wd, eps, alpha,
     with ExitStack() as ctx:
         keep = ctx.enter_context(tc.tile_pool(name="keep", bufs=1))
         turned = ctx.enter_context(tc.psum_pool(name="turned", bufs=4))
-        sums = ctx.enter_context(tc.psum_pool(name="sums", bufs=3))
+        sums = ctx.enter_context(tc.psum_pool(name="sums", bufs=2))
         last = ctx.enter_context(tc.psum_pool(name="last", bufs=1))
+        warm = ctx.enter_context(tc.psum_pool(name="warm", bufs=1))
         ctx.enter_context(tc.manual_schedule())
 
         eps_bc = keep.tile([P, H], BF16)
@@ -84,8 +85,9 @@ def tile_llamamlp_halfwaygin_pa_s_kernel(tc, h_inter, adjacency, Wd, eps, alpha,
         ones_codes = keep.tile([P, WARM_COLUMNS], U32, align_bytes=64)
         ones_scales = keep.tile([P, WARM_COLUMNS], U8, align_bytes=64)
         nc.vector.quantize_mx(out=ones_codes[:].bitcast(FP8X4), scales=ones_scales[:], in_=ones[:])
-        unread = last.tile([P, WARM_COLUMNS], F32, tag="out_ps")
-        for warm_pass in range(WARM_PASSES):
+        unread = warm.tile([P, WARM_COLUMNS], F32)
+
+        def keep_warm():
             nc.tensor.matmul_mx(
                 out=unread[:],
                 lhsT=ones_codes[:, 0:P].bitcast(FP8X4),
@@ -95,6 +97,9 @@ def tile_llamamlp_halfwaygin_pa_s_kernel(tc, h_inter, adjacency, Wd, eps, alpha,
                 start=True,
                 stop=True,
             )
+
+        for warm_pass in range(WARM_PASSES):
+            keep_warm()
 
         wd_grouped = keep.tile([P, D, PACK], BF16, align_bytes=64)
         wd_codes = keep.tile([P, D], U32, align_bytes=64)
@@ -177,6 +182,7 @@ def tile_llamamlp_halfwaygin_pa_s_kernel(tc, h_inter, adjacency, Wd, eps, alpha,
                     start=True,
                     stop=True,
                 )
+            keep_warm()
 
         def mix(x):
             c, pair = divmod(x, 2)

@@ -20,15 +20,15 @@ HD = 128
 D = 128
 C = 4
 PIECES = 2 * C
-QUANTISE_LAG = 2
+QUANTISE_LAG = 1
 MULTIPLY_LAG = 3
-MIX_LAG = 4
-G_TURN_LAG = 7
-G_QUANTISE_LAG = 9
-OUT_LAG = 10
+MIX_LAG = 3
+G_TURN_LAG = 6
+G_QUANTISE_LAG = 8
+OUT_LAG = 9
 RUN = 4
 WARM_COLUMNS = 256
-WARM_PASSES = 8
+WARM_PASSES = 12
 
 FLOPS = 2 * H * S * S * HD + 2 * S * (H * HD) * D
 
@@ -47,7 +47,6 @@ def tile_llamamlp_halfwaygin_pa_s_kernel(tc, h_inter, adjacency, Wd, eps, alpha,
         turned = ctx.enter_context(tc.psum_pool(name="turned", bufs=4))
         sums = ctx.enter_context(tc.psum_pool(name="sums", bufs=2))
         last = ctx.enter_context(tc.psum_pool(name="last", bufs=1))
-        warm = ctx.enter_context(tc.psum_pool(name="warm", bufs=1))
         ctx.enter_context(tc.manual_schedule())
 
         eps_bc = keep.tile([P, H], BF16)
@@ -85,21 +84,21 @@ def tile_llamamlp_halfwaygin_pa_s_kernel(tc, h_inter, adjacency, Wd, eps, alpha,
         ones_codes = keep.tile([P, WARM_COLUMNS], U32, align_bytes=64)
         ones_scales = keep.tile([P, WARM_COLUMNS], U8, align_bytes=64)
         nc.vector.quantize_mx(out=ones_codes[:].bitcast(FP8X4), scales=ones_scales[:], in_=ones[:])
-        unread = warm.tile([P, WARM_COLUMNS], F32)
 
-        def keep_warm():
-            nc.tensor.matmul_mx(
-                out=unread[:],
-                lhsT=ones_codes[:, 0:P].bitcast(FP8X4),
-                lhsT_scale=ones_scales[:, 0:P],
-                rhs=ones_codes[:].bitcast(FP8X4),
-                rhs_scale=ones_scales[:],
-                start=True,
-                stop=True,
-            )
+        def keep_warm(unread, passes):
+            for warm_pass in range(passes):
+                nc.tensor.matmul_mx(
+                    out=unread,
+                    lhsT=ones_codes[:, 0:P].bitcast(FP8X4),
+                    lhsT_scale=ones_scales[:, 0:P],
+                    rhs=ones_codes[:].bitcast(FP8X4),
+                    rhs_scale=ones_scales[:],
+                    start=True,
+                    stop=True,
+                )
 
-        for warm_pass in range(WARM_PASSES):
-            keep_warm()
+        early = last.tile([P, WARM_COLUMNS], F32, tag="out_ps")
+        keep_warm(early[:], WARM_PASSES)
 
         wd_grouped = keep.tile([P, D, PACK], BF16, align_bytes=64)
         wd_codes = keep.tile([P, D], U32, align_bytes=64)
@@ -169,20 +168,21 @@ def tile_llamamlp_halfwaygin_pa_s_kernel(tc, h_inter, adjacency, Wd, eps, alpha,
                 in_=a_grouped[x][:].rearrange("p i s k -> p (i s k)"),
             )
 
-        def multiply(x):
-            agg[x] = sums.tile([P, 2, HD], F32, name="agg", tag="agg")
-            for i in range(2):
-                n = 2 * (x % 2) + i
+        def multiply(c):
+            agg[c] = sums.tile([P, H, HD], F32, name="agg", tag="agg")
+            keep_warm(agg[c][:, 0:2, :].rearrange("p n d -> p (n d)"), 1)
+            for n in range(H):
+                codes, scales = a_codes[2 * c + n // 2], a_scales[2 * c + n // 2]
+                rows = slice(n % 2 * P, (n % 2 + 1) * P)
                 nc.tensor.matmul_mx(
-                    out=agg[x][:, i, :],
-                    lhsT=a_codes[x][:, i * P : (i + 1) * P].bitcast(FP8X4),
-                    lhsT_scale=a_scales[x][:, i * P : (i + 1) * P],
+                    out=agg[c][:, n, :],
+                    lhsT=codes[:, rows].bitcast(FP8X4),
+                    lhsT_scale=scales[:, rows],
                     rhs=h_codes[:, n * HD : (n + 1) * HD].bitcast(FP8X4),
                     rhs_scale=h_scales[:, n * HD : (n + 1) * HD],
                     start=True,
                     stop=True,
                 )
-            keep_warm()
 
         def mix(x):
             c, pair = divmod(x, 2)
@@ -191,7 +191,7 @@ def tile_llamamlp_halfwaygin_pa_s_kernel(tc, h_inter, adjacency, Wd, eps, alpha,
                 cols = slice(n * HD, (n + 1) * HD)
                 nc.vector.scalar_tensor_tensor(
                     out=g_sb[c][:, cols],
-                    in0=agg[x][:, i, :],
+                    in0=agg[c][:, n, :],
                     scalar=alpha_f32[:, n : n + 1],
                     in1=h_term[:, c, cols],
                     op0=MULT,
@@ -205,7 +205,7 @@ def tile_llamamlp_halfwaygin_pa_s_kernel(tc, h_inter, adjacency, Wd, eps, alpha,
         out_rows = out[0].rearrange("(u p e) j -> u e p j", u=2, e=2)
 
         def turn_g(c):
-            g_turned = turned.tile([P, 2, P], F32, tag="turned")
+            g_turned = last.tile([P, 2, P], F32, tag="g_turned")
             row_words = g_sb[c][:].bitcast(F32)
             for u in range(2):
                 nc.tensor.transpose(g_turned[:, u, :], row_words[:, u * P : (u + 1) * P], ident[:])
@@ -242,13 +242,19 @@ def tile_llamamlp_halfwaygin_pa_s_kernel(tc, h_inter, adjacency, Wd, eps, alpha,
             if 0 <= x < PIECES:
                 stage(x)
 
-        def per_slice(stage, twice_c):
-            if twice_c % 2 == 0 and 0 <= twice_c < PIECES:
-                stage(twice_c // 2)
+        def per_slice(stage, x):
+            if x % 2 == 0 and 0 <= x < PIECES:
+                stage(x // 2)
+
+        def turn_slice(c):
+            turn_adjacency(2 * c)
+            turn_adjacency(2 * c + 1)
+            if c < 2:
+                keep_warm(early[:], 2)
 
         for step in range(PIECES + OUT_LAG):
-            per_piece(turn_adjacency, step)
-            per_piece(multiply, step - MULTIPLY_LAG)
+            per_slice(turn_slice, step)
+            per_slice(multiply, step - MULTIPLY_LAG)
             per_piece(quantise_adjacency, step - QUANTISE_LAG)
             per_slice(quantise_g, step - G_QUANTISE_LAG)
             per_slice(project, step - OUT_LAG)

@@ -19,13 +19,7 @@ H = 4
 HD = 128
 D = 128
 C = 4
-PIECES = 2 * C
-QUANTISE_LAG = 1
-MULTIPLY_LAG = 3
-MIX_LAG = 3
-G_TURN_LAG = 6
-G_QUANTISE_LAG = 8
-OUT_LAG = 9
+PIECES = 2 * H
 RUN = 4
 WARM_COLUMNS = 256
 WARM_PASSES = 12
@@ -46,30 +40,35 @@ def tile_llamamlp_halfwaygin_pa_s_kernel(tc, h_inter, adjacency, Wd, eps, alpha,
         keep = ctx.enter_context(tc.tile_pool(name="keep", bufs=1))
         turned = ctx.enter_context(tc.psum_pool(name="turned", bufs=4))
         sums = ctx.enter_context(tc.psum_pool(name="sums", bufs=2))
-        last = ctx.enter_context(tc.psum_pool(name="last", bufs=1))
+        last = ctx.enter_context(tc.psum_pool(name="last", bufs=2))
         ctx.enter_context(tc.manual_schedule())
 
         eps_bc = keep.tile([P, H], BF16)
         nc.scalar.dma_start(out=eps_bc[:], in_=eps.partition_broadcast(P))
         alpha_bc = keep.tile([P, H], BF16)
         nc.scalar.dma_start(out=alpha_bc[:], in_=alpha.partition_broadcast(P))
-        wd_sb = keep.tile([P, PACK, D], BF16)
-        nc.sync.dma_start(
-            out=wd_sb[:].rearrange("p (u e) j -> p u (e j)", u=2),
-            in_=Wd.rearrange("(u p e) j -> p u (e j)", u=2, e=2),
-        )
         h_sb = keep.tile([P, C, H * HD], BF16)
         nc.sync.dma_start(
             out=h_sb[:].rearrange("p (u e) i -> p u (e i)", u=2),
             in_=h_inter[0].rearrange("(u p e) i -> p u (e i)", u=2, e=2),
         )
-        a_rows = adjacency[0].rearrange("n (u p e) t -> u e p n t", u=2, e=2)
         a_sb = []
+        wd_sb = keep.tile([P, PACK, D], BF16)
+        a_heads = adjacency[0].rearrange("n (u p e) t -> u n p (e t)", u=2, e=2)[0]
+        a_slices = adjacency[0].rearrange("n (u p e) t -> u e p n t", u=2, e=2)[1]
         for x in range(PIECES):
-            c, pair = divmod(x, 2)
             a_piece = keep.tile([P, 2, S], BF16, name="a_piece%d" % x)
-            nc.sync.dma_start(out=a_piece[:], in_=a_rows[c // 2, c % 2][:, 2 * pair : 2 * pair + 2, :])
+            if x < H:
+                nc.sync.dma_start(out=a_piece[:].rearrange("p e t -> p (e t)"), in_=a_heads[x])
+            else:
+                c, pair = divmod(x - H, 2)
+                nc.sync.dma_start(out=a_piece[:], in_=a_slices[c][:, 2 * pair : 2 * pair + 2, :])
             a_sb.append(a_piece)
+            if x == H - 1:
+                nc.sync.dma_start(
+                    out=wd_sb[:].rearrange("p (u e) j -> p u (e j)", u=2),
+                    in_=Wd.rearrange("(u p e) j -> p u (e j)", u=2, e=2),
+                )
 
         zero = keep.tile([P, 1], F32)
         nc.vector.memset(zero[:], 0.0)
@@ -100,34 +99,11 @@ def tile_llamamlp_halfwaygin_pa_s_kernel(tc, h_inter, adjacency, Wd, eps, alpha,
         early = last.tile([P, WARM_COLUMNS], F32, tag="out_ps")
         keep_warm(early[:], WARM_PASSES)
 
-        wd_grouped = keep.tile([P, D, PACK], BF16, align_bytes=64)
-        wd_codes = keep.tile([P, D], U32, align_bytes=64)
-        wd_scales = keep.tile([P, D], U8, align_bytes=64)
-        regroup(nc.vector.tensor_copy, wd_grouped[:], wd_sb[:])
-
         one_plus_eps = keep.tile([P, H], F32)
         nc.vector.tensor_scalar_add(out=one_plus_eps[:], in0=eps_bc[:], scalar1=1.0)
-        alpha_f32 = keep.tile([P, H], F32)
-        nc.vector.tensor_copy(out=alpha_f32[:], in_=alpha_bc[:])
-
-        nc.vector.quantize_mx(
-            out=wd_codes[:].bitcast(FP8X4),
-            scales=wd_scales[:],
-            in_=wd_grouped[:].rearrange("p j k -> p (j k)"),
-        )
-
-        h_grouped = keep.tile([P, H * HD, PACK], BF16, align_bytes=64)
-        h_codes = keep.tile([P, H * HD], U32, align_bytes=64)
-        h_scales = keep.tile([P, H * HD], U8, align_bytes=64)
-        regroup(nc.vector.tensor_copy, h_grouped[:], h_sb[:])
-        nc.vector.quantize_mx(
-            out=h_codes[:].bitcast(FP8X4),
-            scales=h_scales[:],
-            in_=h_grouped[:].rearrange("p i c -> p (i c)"),
-        )
-
         h_term = keep.tile([P, C, H * HD], F32)
-        for n in range(H):
+
+        def scale_h(n):
             cols = slice(n * HD, (n + 1) * HD)
             if n < H - 1:
                 nc.scalar.activation(
@@ -138,25 +114,49 @@ def tile_llamamlp_halfwaygin_pa_s_kernel(tc, h_inter, adjacency, Wd, eps, alpha,
                     out=h_term[:, :, cols], in0=h_sb[:, :, cols], scalar1=one_plus_eps[:, n : n + 1]
                 )
 
+        h_grouped = keep.tile([P, H * HD, PACK], BF16, align_bytes=64)
+        h_codes = keep.tile([P, H * HD], U32, align_bytes=64)
+        h_scales = keep.tile([P, H * HD], U8, align_bytes=64)
+
+        def quantise_h():
+            regroup(nc.vector.tensor_copy, h_grouped[:], h_sb[:])
+            nc.vector.quantize_mx(
+                out=h_codes[:].bitcast(FP8X4),
+                scales=h_scales[:],
+                in_=h_grouped[:].rearrange("p i c -> p (i c)"),
+            )
+
+        wd_grouped = keep.tile([P, D, PACK], BF16, align_bytes=64)
+        wd_codes = keep.tile([P, D], U32, align_bytes=64)
+        wd_scales = keep.tile([P, D], U8, align_bytes=64)
+
+        def quantise_wd():
+            regroup(nc.vector.tensor_copy, wd_grouped[:], wd_sb[:])
+            nc.vector.quantize_mx(
+                out=wd_codes[:].bitcast(FP8X4),
+                scales=wd_scales[:],
+                in_=wd_grouped[:].rearrange("p j k -> p (j k)"),
+            )
+
         a_grouped = {}
         a_codes = {}
         a_scales = {}
         agg = {}
-        g_sb = [keep.tile([P, H * HD], BF16, align_bytes=64, name="g_sb%d" % c) for c in range(C)]
+        g_sb = {c: keep.tile([P, 2 if c == 0 else 1, H * HD], BF16, align_bytes=64, name="g_sb%d" % c) for c in (0, 2, 3)}
 
         def turn_adjacency(x):
             a_turned = turned.tile([P, 2, 2, P], F32, tag="turned")
-            for i in range(2):
-                row_words = a_sb[x][:, i, :].bitcast(F32)
+            for r in range(2):
+                row_words = a_sb[x][:, r, :].bitcast(F32)
                 for u in range(2):
-                    nc.tensor.transpose(a_turned[:, i, u, :], row_words[:, u * P : (u + 1) * P], ident[:])
+                    nc.tensor.transpose(a_turned[:, r, u, :], row_words[:, u * P : (u + 1) * P], ident[:])
             a_grouped[x] = keep.tile([P, 2, P, PACK], BF16, align_bytes=64, name="a_grouped%d" % x)
             nc.scalar.copy(
                 out=a_grouped[x][:]
-                .rearrange("p i s k -> p (i s k)")
+                .rearrange("p r s k -> p (r s k)")
                 .bitcast(F32)
-                .rearrange("p (i s u) -> p i s u", i=2, u=2),
-                in_=a_turned[:].rearrange("p i u s -> p i s u"),
+                .rearrange("p (r s u) -> p r s u", r=2, u=2),
+                in_=a_turned[:].rearrange("p r u s -> p r s u"),
             )
 
         def quantise_adjacency(x):
@@ -165,98 +165,138 @@ def tile_llamamlp_halfwaygin_pa_s_kernel(tc, h_inter, adjacency, Wd, eps, alpha,
             nc.vector.quantize_mx(
                 out=a_codes[x][:].bitcast(FP8X4),
                 scales=a_scales[x][:],
-                in_=a_grouped[x][:].rearrange("p i s k -> p (i s k)"),
+                in_=a_grouped[x][:].rearrange("p r s k -> p (r s k)"),
             )
 
-        def multiply(c):
-            agg[c] = sums.tile([P, H, HD], F32, name="agg", tag="agg")
-            keep_warm(agg[c][:, 0:2, :].rearrange("p n d -> p (n d)"), 1)
-            for n in range(H):
-                codes, scales = a_codes[2 * c + n // 2], a_scales[2 * c + n // 2]
-                rows = slice(n % 2 * P, (n % 2 + 1) * P)
-                nc.tensor.matmul_mx(
-                    out=agg[c][:, n, :],
-                    lhsT=codes[:, rows].bitcast(FP8X4),
-                    lhsT_scale=scales[:, rows],
-                    rhs=h_codes[:, n * HD : (n + 1) * HD].bitcast(FP8X4),
-                    rhs_scale=h_scales[:, n * HD : (n + 1) * HD],
-                    start=True,
-                    stop=True,
-                )
+        def head_of(x, r):
+            return x if x < H else 2 * (x % 2) + r
+
+        def multiply(k):
+            agg[k] = sums.tile([P, 2, 2, HD], F32, name="agg", tag="agg")
+            keep_warm(agg[k][:, 0].rearrange("p r d -> p (r d)"), 1)
+            for x in (2 * k, 2 * k + 1):
+                for r in range(2):
+                    n = head_of(x, r)
+                    nc.tensor.matmul_mx(
+                        out=agg[k][:, x % 2, r, :],
+                        lhsT=a_codes[x][:, r * P : (r + 1) * P].bitcast(FP8X4),
+                        lhsT_scale=a_scales[x][:, r * P : (r + 1) * P],
+                        rhs=h_codes[:, n * HD : (n + 1) * HD].bitcast(FP8X4),
+                        rhs_scale=h_scales[:, n * HD : (n + 1) * HD],
+                        start=True,
+                        stop=True,
+                    )
 
         def mix(x):
-            c, pair = divmod(x, 2)
-            for i in range(2):
-                n = 2 * pair + i
-                cols = slice(n * HD, (n + 1) * HD)
+            if x < H:
+                cols = slice(x * HD, (x + 1) * HD)
+                parts = [(x, g_sb[0][:, :, cols], agg[x // 2][:, x % 2], h_term[:, 0:2, cols])]
+            else:
+                c = x // 2
+                parts = []
+                for r in range(2):
+                    n = head_of(x, r)
+                    cols = slice(n * HD, (n + 1) * HD)
+                    parts.append((n, g_sb[c][:, 0, cols], agg[c][:, x % 2, r, :], h_term[:, c, cols]))
+            for n, g_part, agg_part, h_part in parts:
                 nc.vector.scalar_tensor_tensor(
-                    out=g_sb[c][:, cols],
-                    in0=agg[c][:, n, :],
-                    scalar=alpha_f32[:, n : n + 1],
-                    in1=h_term[:, c, cols],
-                    op0=MULT,
-                    op1=ADD,
+                    out=g_part, in0=agg_part, scalar=alpha_bc[:, n : n + 1], in1=h_part, op0=MULT, op1=ADD
                 )
 
         g_grouped = {}
         g_codes = {}
         g_scales = {}
         out_sb = keep.tile([P, C, D], F32)
-        out_rows = out[0].rearrange("(u p e) j -> u e p j", u=2, e=2)
+        out_rows = out[0].rearrange("(u p e) j -> u p e j", u=2, e=2)
+
+        def slices_of(c):
+            return 2 if c == 0 else 1
 
         def turn_g(c):
-            g_turned = last.tile([P, 2, P], F32, tag="g_turned")
-            row_words = g_sb[c][:].bitcast(F32)
-            for u in range(2):
-                nc.tensor.transpose(g_turned[:, u, :], row_words[:, u * P : (u + 1) * P], ident[:])
-            g_grouped[c] = keep.tile([P, P, PACK], BF16, align_bytes=64, name="g_grouped%d" % c)
+            count = slices_of(c)
+            g_turned = turned.tile([P, count, 2, P], F32, tag="turned")
+            for r in range(count):
+                row_words = g_sb[c][:, r, :].bitcast(F32)
+                for u in range(2):
+                    nc.tensor.transpose(g_turned[:, r, u, :], row_words[:, u * P : (u + 1) * P], ident[:])
+            g_grouped[c] = keep.tile([P, count, P, PACK], BF16, align_bytes=64, name="g_grouped%d" % c)
             nc.scalar.copy(
-                out=g_grouped[c][:].rearrange("p s k -> p (s k)").bitcast(F32).rearrange("p (s u) -> p s u", u=2),
-                in_=g_turned[:].rearrange("p u s -> p s u"),
+                out=g_grouped[c][:]
+                .rearrange("p r s k -> p (r s k)")
+                .bitcast(F32)
+                .rearrange("p (r s u) -> p r s u", r=count, u=2),
+                in_=g_turned[:].rearrange("p r u s -> p r s u"),
             )
 
         def quantise_g(c):
-            g_codes[c] = keep.tile([P, P], U32, align_bytes=64, name="g_codes%d" % c)
-            g_scales[c] = keep.tile([P, P], U8, align_bytes=64, name="g_scales%d" % c)
+            count = slices_of(c)
+            g_codes[c] = keep.tile([P, count * P], U32, align_bytes=64, name="g_codes%d" % c)
+            g_scales[c] = keep.tile([P, count * P], U8, align_bytes=64, name="g_scales%d" % c)
             nc.vector.quantize_mx(
                 out=g_codes[c][:].bitcast(FP8X4),
                 scales=g_scales[c][:],
-                in_=g_grouped[c][:].rearrange("p s k -> p (s k)"),
+                in_=g_grouped[c][:].rearrange("p r s k -> p (r s k)"),
             )
 
         def project(c):
-            out_ps = last.tile([P, D], F32, tag="out_ps")
-            nc.tensor.matmul_mx(
-                out=out_ps[:],
-                lhsT=g_codes[c][:].bitcast(FP8X4),
-                lhsT_scale=g_scales[c][:],
-                rhs=wd_codes[:].bitcast(FP8X4),
-                rhs_scale=wd_scales[:],
-                start=True,
-                stop=True,
-            )
-            nc.scalar.copy(out=out_sb[:, c, :], in_=out_ps[:])
-            nc.sync.dma_start(out=out_rows[c // 2, c % 2], in_=out_sb[:, c, :])
+            count = slices_of(c)
+            out_ps = last.tile([P, count, D], F32, tag="out_ps")
+            for r in range(count):
+                nc.tensor.matmul_mx(
+                    out=out_ps[:, r, :],
+                    lhsT=g_codes[c][:, r * P : (r + 1) * P].bitcast(FP8X4),
+                    lhsT_scale=g_scales[c][:, r * P : (r + 1) * P],
+                    rhs=wd_codes[:].bitcast(FP8X4),
+                    rhs_scale=wd_scales[:],
+                    start=True,
+                    stop=True,
+                )
+            nc.scalar.copy(out=out_sb[:, c : c + count, :], in_=out_ps[:])
+            u, e = divmod(c, 2)
+            nc.sync.dma_start(out=out_rows[u][:, e : e + count, :], in_=out_sb[:, c : c + count, :])
 
-        def per_piece(stage, x):
-            if 0 <= x < PIECES:
-                stage(x)
-
-        def per_slice(stage, x):
-            if x % 2 == 0 and 0 <= x < PIECES:
-                stage(x // 2)
-
-        def turn_slice(c):
-            turn_adjacency(2 * c)
-            turn_adjacency(2 * c + 1)
-            if c < 2:
-                keep_warm(early[:], 2)
-
-        for step in range(PIECES + OUT_LAG):
-            per_slice(turn_slice, step)
-            per_slice(multiply, step - MULTIPLY_LAG)
-            per_piece(quantise_adjacency, step - QUANTISE_LAG)
-            per_slice(quantise_g, step - G_QUANTISE_LAG)
-            per_slice(project, step - OUT_LAG)
-            per_piece(mix, step - MIX_LAG)
-            per_slice(turn_g, step - G_TURN_LAG)
+        scale_h(0)
+        scale_h(1)
+        quantise_h()
+        scale_h(3)
+        turn_adjacency(0)
+        turn_adjacency(1)
+        keep_warm(early[:], 2)
+        scale_h(2)
+        turn_adjacency(2)
+        turn_adjacency(3)
+        keep_warm(early[:], 2)
+        quantise_adjacency(0)
+        quantise_adjacency(1)
+        quantise_wd()
+        multiply(0)
+        quantise_adjacency(2)
+        quantise_adjacency(3)
+        turn_adjacency(4)
+        turn_adjacency(5)
+        mix(0)
+        mix(1)
+        multiply(1)
+        quantise_adjacency(4)
+        quantise_adjacency(5)
+        turn_adjacency(6)
+        turn_adjacency(7)
+        mix(2)
+        mix(3)
+        multiply(2)
+        turn_g(0)
+        quantise_adjacency(6)
+        mix(4)
+        quantise_adjacency(7)
+        mix(5)
+        multiply(3)
+        turn_g(2)
+        quantise_g(0)
+        project(0)
+        mix(6)
+        mix(7)
+        turn_g(3)
+        quantise_g(2)
+        quantise_g(3)
+        project(2)
+        project(3)

@@ -22,7 +22,7 @@ C = 4
 PIECES = 2 * H
 RUN = 4
 WARM_COLUMNS = 256
-WARM_PASSES = 12
+WARM_PASSES = 8
 
 FLOPS = 2 * H * S * S * HD + 2 * S * (H * HD) * D
 
@@ -64,11 +64,10 @@ def tile_llamamlp_halfwaygin_pa_s_kernel(tc, h_inter, adjacency, Wd, eps, alpha,
                 c, pair = divmod(x - H, 2)
                 nc.sync.dma_start(out=a_piece[:], in_=a_slices[c][:, 2 * pair : 2 * pair + 2, :])
             a_sb.append(a_piece)
-            if x == H - 1:
-                nc.sync.dma_start(
-                    out=wd_sb[:].rearrange("p (u e) j -> p u (e j)", u=2),
-                    in_=Wd.rearrange("(u p e) j -> p u (e j)", u=2, e=2),
-                )
+        nc.sync.dma_start(
+            out=wd_sb[:].rearrange("p (u e) j -> p u (e j)", u=2),
+            in_=Wd.rearrange("(u p e) j -> p u (e j)", u=2, e=2),
+        )
 
         zero = keep.tile([P, 1], F32)
         nc.vector.memset(zero[:], 0.0)
@@ -78,20 +77,20 @@ def tile_llamamlp_halfwaygin_pa_s_kernel(tc, h_inter, adjacency, Wd, eps, alpha,
         ident = keep.tile([P, P], F32)
         make_identity(nc, ident[:])
 
-        ones = keep.tile([P, WARM_COLUMNS * PACK], BF16, align_bytes=64)
-        nc.vector.memset(ones[:], 1.0)
-        ones_codes = keep.tile([P, WARM_COLUMNS], U32, align_bytes=64)
-        ones_scales = keep.tile([P, WARM_COLUMNS], U8, align_bytes=64)
-        nc.vector.quantize_mx(out=ones_codes[:].bitcast(FP8X4), scales=ones_scales[:], in_=ones[:])
+        idle = keep.tile([P, WARM_COLUMNS * PACK], BF16, align_bytes=64)
+        nc.vector.memset(idle[:].bitcast(U32), 0)
+        idle_codes = keep.tile([P, WARM_COLUMNS], U32, align_bytes=64)
+        idle_scales = keep.tile([P, WARM_COLUMNS], U8, align_bytes=64)
+        nc.vector.quantize_mx(out=idle_codes[:].bitcast(FP8X4), scales=idle_scales[:], in_=idle[:])
 
         def keep_warm(unread, passes):
             for warm_pass in range(passes):
                 nc.tensor.matmul_mx(
                     out=unread,
-                    lhsT=ones_codes[:, 0:P].bitcast(FP8X4),
-                    lhsT_scale=ones_scales[:, 0:P],
-                    rhs=ones_codes[:].bitcast(FP8X4),
-                    rhs_scale=ones_scales[:],
+                    lhsT=idle_codes[:, 0:P].bitcast(FP8X4),
+                    lhsT_scale=idle_scales[:, 0:P],
+                    rhs=idle_codes[:].bitcast(FP8X4),
+                    rhs_scale=idle_scales[:],
                     start=True,
                     stop=True,
                 )
@@ -119,19 +118,24 @@ def tile_llamamlp_halfwaygin_pa_s_kernel(tc, h_inter, adjacency, Wd, eps, alpha,
         h_scales = keep.tile([P, H * HD], U8, align_bytes=64)
 
         def quantise_h():
-            regroup(nc.vector.tensor_copy, h_grouped[:], h_sb[:])
-            nc.vector.quantize_mx(
-                out=h_codes[:].bitcast(FP8X4),
-                scales=h_scales[:],
-                in_=h_grouped[:].rearrange("p i c -> p (i c)"),
-            )
+            halves = [slice(0, H * HD // 2), slice(H * HD // 2, H * HD)]
+            for cols in halves:
+                regroup(nc.vector.tensor_copy, h_grouped[:, cols, :], h_sb[:, :, cols])
+            for cols in halves:
+                nc.vector.quantize_mx(
+                    out=h_codes[:, cols].bitcast(FP8X4),
+                    scales=h_scales[:, cols],
+                    in_=h_grouped[:, cols, :].rearrange("p i c -> p (i c)"),
+                )
 
         wd_grouped = keep.tile([P, D, PACK], BF16, align_bytes=64)
         wd_codes = keep.tile([P, D], U32, align_bytes=64)
         wd_scales = keep.tile([P, D], U8, align_bytes=64)
 
-        def quantise_wd():
+        def regroup_wd():
             regroup(nc.vector.tensor_copy, wd_grouped[:], wd_sb[:])
+
+        def quantise_wd():
             nc.vector.quantize_mx(
                 out=wd_codes[:].bitcast(FP8X4),
                 scales=wd_scales[:],
@@ -173,7 +177,8 @@ def tile_llamamlp_halfwaygin_pa_s_kernel(tc, h_inter, adjacency, Wd, eps, alpha,
 
         def multiply(k):
             agg[k] = sums.tile([P, 2, 2, HD], F32, name="agg", tag="agg")
-            keep_warm(agg[k][:, 0].rearrange("p r d -> p (r d)"), 1)
+            if k < 3:
+                keep_warm(agg[k][:, 0].rearrange("p r d -> p (r d)"), 1)
             for x in (2 * k, 2 * k + 1):
                 for r in range(2):
                     n = head_of(x, r)
@@ -258,36 +263,37 @@ def tile_llamamlp_halfwaygin_pa_s_kernel(tc, h_inter, adjacency, Wd, eps, alpha,
         scale_h(0)
         scale_h(1)
         quantise_h()
-        scale_h(3)
         turn_adjacency(0)
         turn_adjacency(1)
         keep_warm(early[:], 2)
-        scale_h(2)
+        quantise_adjacency(0)
+        quantise_adjacency(1)
+        scale_h(3)
         turn_adjacency(2)
         turn_adjacency(3)
         keep_warm(early[:], 2)
-        quantise_adjacency(0)
-        quantise_adjacency(1)
-        quantise_wd()
-        multiply(0)
+        scale_h(2)
         quantise_adjacency(2)
         quantise_adjacency(3)
         turn_adjacency(4)
-        turn_adjacency(5)
+        multiply(0)
         mix(0)
         mix(1)
-        multiply(1)
+        turn_adjacency(5)
         quantise_adjacency(4)
+        multiply(1)
+        mix(2)
+        mix(3)
         quantise_adjacency(5)
         turn_adjacency(6)
         turn_adjacency(7)
-        mix(2)
-        mix(3)
-        multiply(2)
         turn_g(0)
+        regroup_wd()
         quantise_adjacency(6)
-        mix(4)
+        quantise_wd()
         quantise_adjacency(7)
+        multiply(2)
+        mix(4)
         mix(5)
         multiply(3)
         turn_g(2)

@@ -22,7 +22,9 @@ C = 4
 PIECES = 2 * H
 RUN = 4
 WARM_COLUMNS = 256
-WARM_PASSES = 8
+WARM_PASSES = 12
+
+TWO_ONES = 0x3F803F80
 
 FLOPS = 2 * H * S * S * HD + 2 * S * (H * HD) * D
 
@@ -78,7 +80,7 @@ def tile_llamamlp_halfwaygin_pa_s_kernel(tc, h_inter, adjacency, Wd, eps, alpha,
         make_identity(nc, ident[:])
 
         idle = keep.tile([P, WARM_COLUMNS * PACK], BF16, align_bytes=64)
-        nc.vector.memset(idle[:].bitcast(U32), 0)
+        nc.vector.memset(idle[:].bitcast(U32), TWO_ONES)
         idle_codes = keep.tile([P, WARM_COLUMNS], U32, align_bytes=64)
         idle_scales = keep.tile([P, WARM_COLUMNS], U8, align_bytes=64)
         nc.vector.quantize_mx(out=idle_codes[:].bitcast(FP8X4), scales=idle_scales[:], in_=idle[:])
@@ -177,8 +179,7 @@ def tile_llamamlp_halfwaygin_pa_s_kernel(tc, h_inter, adjacency, Wd, eps, alpha,
 
         def multiply(k):
             agg[k] = sums.tile([P, 2, 2, HD], F32, name="agg", tag="agg")
-            if k < 3:
-                keep_warm(agg[k][:, 0].rearrange("p r d -> p (r d)"), 1)
+            keep_warm(agg[k][:, 0].rearrange("p r d -> p (r d)"), 2 if k == 3 else 1)
             for x in (2 * k, 2 * k + 1):
                 for r in range(2):
                     n = head_of(x, r)
@@ -265,13 +266,12 @@ def tile_llamamlp_halfwaygin_pa_s_kernel(tc, h_inter, adjacency, Wd, eps, alpha,
         quantise_h()
         turn_adjacency(0)
         turn_adjacency(1)
-        keep_warm(early[:], 2)
         quantise_adjacency(0)
         quantise_adjacency(1)
         scale_h(3)
         turn_adjacency(2)
+        keep_warm(early[:], 4)
         turn_adjacency(3)
-        keep_warm(early[:], 2)
         scale_h(2)
         quantise_adjacency(2)
         quantise_adjacency(3)
@@ -287,6 +287,7 @@ def tile_llamamlp_halfwaygin_pa_s_kernel(tc, h_inter, adjacency, Wd, eps, alpha,
         quantise_adjacency(5)
         turn_adjacency(6)
         turn_adjacency(7)
+        keep_warm(early[:], 2)
         turn_g(0)
         regroup_wd()
         quantise_adjacency(6)

@@ -19,7 +19,12 @@ H = 4
 HD = 128
 D = 128
 C = 4
-PIECES = 2 * H
+PAIRED = H + 2
+PIECES = [[(k % H, 2 * (k // H)), (k % H, 2 * (k // H) + 1)] for k in range(PAIRED)] + [
+    [(2, 2), (3, 2)],
+    [(2, 3)],
+    [(3, 3)],
+]
 RUN = 4
 WARM_COLUMNS = 256
 WARM_PASSES = 12
@@ -45,27 +50,28 @@ def tile_llamamlp_halfwaygin_pa_s_kernel(tc, h_inter, adjacency, Wd, eps, alpha,
         last = ctx.enter_context(tc.psum_pool(name="last", bufs=2))
         ctx.enter_context(tc.manual_schedule())
 
-        eps_bc = keep.tile([P, H], BF16)
-        nc.scalar.dma_start(out=eps_bc[:], in_=eps.partition_broadcast(P))
-        alpha_bc = keep.tile([P, H], BF16)
-        nc.scalar.dma_start(out=alpha_bc[:], in_=alpha.partition_broadcast(P))
         h_sb = keep.tile([P, C, H * HD], BF16)
         nc.sync.dma_start(
             out=h_sb[:].rearrange("p (u e) i -> p u (e i)", u=2),
             in_=h_inter[0].rearrange("(u p e) i -> p u (e i)", u=2, e=2),
         )
+        a_pairs = adjacency[0].rearrange("n (u p e) t -> u n p (e t)", u=2, e=2)
+        a_rows = adjacency[0].rearrange("n (u p e) t -> u e p n t", u=2, e=2)
         a_sb = []
-        wd_sb = keep.tile([P, PACK, D], BF16)
-        a_heads = adjacency[0].rearrange("n (u p e) t -> u n p (e t)", u=2, e=2)[0]
-        a_slices = adjacency[0].rearrange("n (u p e) t -> u e p n t", u=2, e=2)[1]
-        for x in range(PIECES):
-            a_piece = keep.tile([P, 2, S], BF16, name="a_piece%d" % x)
-            if x < H:
-                nc.sync.dma_start(out=a_piece[:].rearrange("p e t -> p (e t)"), in_=a_heads[x])
+        eps_bc = keep.tile([P, H], BF16)
+        alpha_bc = keep.tile([P, H], BF16)
+        for x, blocks in enumerate(PIECES):
+            n, c = blocks[0]
+            a_piece = keep.tile([P, len(blocks), S], BF16, name="a_piece%d" % x)
+            if x < PAIRED:
+                nc.sync.dma_start(out=a_piece[:].rearrange("p e t -> p (e t)"), in_=a_pairs[c // 2, n])
             else:
-                c, pair = divmod(x - H, 2)
-                nc.sync.dma_start(out=a_piece[:], in_=a_slices[c][:, 2 * pair : 2 * pair + 2, :])
+                nc.sync.dma_start(out=a_piece[:], in_=a_rows[c // 2, c % 2][:, n : n + len(blocks), :])
             a_sb.append(a_piece)
+            if x == 0:
+                nc.scalar.dma_start(out=eps_bc[:], in_=eps.partition_broadcast(P))
+                nc.scalar.dma_start(out=alpha_bc[:], in_=alpha.partition_broadcast(P))
+        wd_sb = keep.tile([P, PACK, D], BF16)
         nc.sync.dma_start(
             out=wd_sb[:].rearrange("p (u e) j -> p u (e j)", u=2),
             in_=Wd.rearrange("(u p e) j -> p u (e j)", u=2, e=2),
@@ -135,7 +141,7 @@ def tile_llamamlp_halfwaygin_pa_s_kernel(tc, h_inter, adjacency, Wd, eps, alpha,
         wd_scales = keep.tile([P, D], U8, align_bytes=64)
 
         def regroup_wd():
-            regroup(nc.vector.tensor_copy, wd_grouped[:], wd_sb[:])
+            regroup(nc.scalar.copy, wd_grouped[:], wd_sb[:])
 
         def quantise_wd():
             nc.vector.quantize_mx(
@@ -148,43 +154,43 @@ def tile_llamamlp_halfwaygin_pa_s_kernel(tc, h_inter, adjacency, Wd, eps, alpha,
         a_codes = {}
         a_scales = {}
         agg = {}
-        g_sb = {c: keep.tile([P, 2 if c == 0 else 1, H * HD], BF16, align_bytes=64, name="g_sb%d" % c) for c in (0, 2, 3)}
+        g_sb = [keep.tile([P, 2, H * HD], BF16, align_bytes=64, name="g_sb%d" % u) for u in range(2)]
 
         def turn_adjacency(x):
-            a_turned = turned.tile([P, 2, 2, P], F32, tag="turned")
-            for r in range(2):
+            count = len(PIECES[x])
+            a_turned = turned.tile([P, count, 2, P], F32, tag="turned")
+            for r in range(count):
                 row_words = a_sb[x][:, r, :].bitcast(F32)
                 for u in range(2):
                     nc.tensor.transpose(a_turned[:, r, u, :], row_words[:, u * P : (u + 1) * P], ident[:])
-            a_grouped[x] = keep.tile([P, 2, P, PACK], BF16, align_bytes=64, name="a_grouped%d" % x)
+            a_grouped[x] = keep.tile([P, count, P, PACK], BF16, align_bytes=64, name="a_grouped%d" % x)
             nc.scalar.copy(
                 out=a_grouped[x][:]
                 .rearrange("p r s k -> p (r s k)")
                 .bitcast(F32)
-                .rearrange("p (r s u) -> p r s u", r=2, u=2),
+                .rearrange("p (r s u) -> p r s u", r=count, u=2),
                 in_=a_turned[:].rearrange("p r u s -> p r s u"),
             )
 
         def quantise_adjacency(x):
-            a_codes[x] = keep.tile([P, 2 * P], U32, align_bytes=64, name="a_codes%d" % x)
-            a_scales[x] = keep.tile([P, 2 * P], U8, align_bytes=64, name="a_scales%d" % x)
+            count = len(PIECES[x])
+            a_codes[x] = keep.tile([P, count * P], U32, align_bytes=64, name="a_codes%d" % x)
+            a_scales[x] = keep.tile([P, count * P], U8, align_bytes=64, name="a_scales%d" % x)
             nc.vector.quantize_mx(
                 out=a_codes[x][:].bitcast(FP8X4),
                 scales=a_scales[x][:],
                 in_=a_grouped[x][:].rearrange("p r s k -> p (r s k)"),
             )
 
-        def head_of(x, r):
-            return x if x < H else 2 * (x % 2) + r
-
-        def multiply(k):
-            agg[k] = sums.tile([P, 2, 2, HD], F32, name="agg", tag="agg")
-            keep_warm(agg[k][:, 0].rearrange("p r d -> p (r d)"), 2 if k == 3 else 1)
-            for x in (2 * k, 2 * k + 1):
-                for r in range(2):
-                    n = head_of(x, r)
+        def multiply(pieces, warm_passes):
+            bank = sums.tile([P, 4, HD], F32, name="bank", tag="bank")
+            keep_warm(bank[:, 0:2, :].rearrange("p r d -> p (r d)"), warm_passes)
+            place = 0
+            for x in pieces:
+                agg[x] = bank[:, place : place + len(PIECES[x]), :]
+                for r, (n, c) in enumerate(PIECES[x]):
                     nc.tensor.matmul_mx(
-                        out=agg[k][:, x % 2, r, :],
+                        out=bank[:, place, :],
                         lhsT=a_codes[x][:, r * P : (r + 1) * P].bitcast(FP8X4),
                         lhsT_scale=a_scales[x][:, r * P : (r + 1) * P],
                         rhs=h_codes[:, n * HD : (n + 1) * HD].bitcast(FP8X4),
@@ -192,21 +198,21 @@ def tile_llamamlp_halfwaygin_pa_s_kernel(tc, h_inter, adjacency, Wd, eps, alpha,
                         start=True,
                         stop=True,
                     )
+                    place += 1
 
         def mix(x):
-            if x < H:
-                cols = slice(x * HD, (x + 1) * HD)
-                parts = [(x, g_sb[0][:, :, cols], agg[x // 2][:, x % 2], h_term[:, 0:2, cols])]
+            n, c = PIECES[x][0]
+            if x < PAIRED:
+                cols = slice(n * HD, (n + 1) * HD)
+                parts = [(n, g_sb[c // 2][:, :, cols], agg[x], h_term[:, c : c + 2, cols])]
             else:
-                c = x // 2
                 parts = []
-                for r in range(2):
-                    n = head_of(x, r)
-                    cols = slice(n * HD, (n + 1) * HD)
-                    parts.append((n, g_sb[c][:, 0, cols], agg[c][:, x % 2, r, :], h_term[:, c, cols]))
-            for n, g_part, agg_part, h_part in parts:
+                for r in range(len(PIECES[x])):
+                    cols = slice((n + r) * HD, (n + r + 1) * HD)
+                    parts.append((n + r, g_sb[c // 2][:, c % 2, cols], agg[x][:, r, :], h_term[:, c, cols]))
+            for head, g_part, agg_part, h_part in parts:
                 nc.vector.scalar_tensor_tensor(
-                    out=g_part, in0=agg_part, scalar=alpha_bc[:, n : n + 1], in1=h_part, op0=MULT, op1=ADD
+                    out=g_part, in0=agg_part, scalar=alpha_bc[:, head : head + 1], in1=h_part, op0=MULT, op1=ADD
                 )
 
         g_grouped = {}
@@ -222,7 +228,7 @@ def tile_llamamlp_halfwaygin_pa_s_kernel(tc, h_inter, adjacency, Wd, eps, alpha,
             count = slices_of(c)
             g_turned = turned.tile([P, count, 2, P], F32, tag="turned")
             for r in range(count):
-                row_words = g_sb[c][:, r, :].bitcast(F32)
+                row_words = g_sb[c // 2][:, c % 2 + r, :].bitcast(F32)
                 for u in range(2):
                     nc.tensor.transpose(g_turned[:, r, u, :], row_words[:, u * P : (u + 1) * P], ident[:])
             g_grouped[c] = keep.tile([P, count, P, PACK], BF16, align_bytes=64, name="g_grouped%d" % c)
@@ -263,47 +269,50 @@ def tile_llamamlp_halfwaygin_pa_s_kernel(tc, h_inter, adjacency, Wd, eps, alpha,
 
         scale_h(0)
         scale_h(1)
+        scale_h(2)
         quantise_h()
         turn_adjacency(0)
         turn_adjacency(1)
+        turn_adjacency(2)
+        keep_warm(early[:], 4)
         quantise_adjacency(0)
         quantise_adjacency(1)
         scale_h(3)
-        turn_adjacency(2)
-        keep_warm(early[:], 4)
         turn_adjacency(3)
-        scale_h(2)
+        turn_adjacency(4)
         quantise_adjacency(2)
         quantise_adjacency(3)
-        turn_adjacency(4)
-        multiply(0)
+        multiply((0, 1), 1)
         mix(0)
         mix(1)
         turn_adjacency(5)
         quantise_adjacency(4)
-        multiply(1)
+        quantise_adjacency(5)
+        multiply((2, 3), 1)
         mix(2)
         mix(3)
-        quantise_adjacency(5)
         turn_adjacency(6)
         turn_adjacency(7)
-        keep_warm(early[:], 2)
-        turn_g(0)
+        turn_adjacency(8)
         regroup_wd()
         quantise_adjacency(6)
-        quantise_wd()
         quantise_adjacency(7)
-        multiply(2)
+        multiply((4, 5), 2)
         mix(4)
+        quantise_adjacency(8)
         mix(5)
-        multiply(3)
-        turn_g(2)
-        quantise_g(0)
-        project(0)
+        turn_g(0)
+        multiply((6, 7, 8), 0)
+        keep_warm(early[:], 2)
         mix(6)
         mix(7)
+        mix(8)
+        turn_g(2)
         turn_g(3)
+        quantise_g(0)
+        quantise_wd()
         quantise_g(2)
         quantise_g(3)
+        project(0)
         project(2)
         project(3)

@@ -27,7 +27,7 @@ PIECES = [[(k % H, 2 * (k // H)), (k % H, 2 * (k // H) + 1)] for k in range(PAIR
 ]
 RUN = 4
 WARM_COLUMNS = 256
-WARM_PASSES = 12
+WARM_PASSES = 13
 
 TWO_ONES = 0x3F803F80
 
@@ -273,8 +273,8 @@ def tile_llamamlp_halfwaygin_pa_s_kernel(tc, h_inter, adjacency, Wd, eps, alpha,
         quantise_h()
         turn_adjacency(0)
         turn_adjacency(1)
-        turn_adjacency(2)
         keep_warm(early[:], 4)
+        turn_adjacency(2)
         quantise_adjacency(0)
         quantise_adjacency(1)
         scale_h(3)
@@ -282,16 +282,16 @@ def tile_llamamlp_halfwaygin_pa_s_kernel(tc, h_inter, adjacency, Wd, eps, alpha,
         turn_adjacency(4)
         quantise_adjacency(2)
         quantise_adjacency(3)
-        multiply((0, 1), 1)
+        multiply((0, 1), 2)
         mix(0)
         mix(1)
         turn_adjacency(5)
+        turn_adjacency(6)
         quantise_adjacency(4)
         quantise_adjacency(5)
         multiply((2, 3), 1)
         mix(2)
         mix(3)
-        turn_adjacency(6)
         turn_adjacency(7)
         turn_adjacency(8)
         regroup_wd()
@@ -302,7 +302,7 @@ def tile_llamamlp_halfwaygin_pa_s_kernel(tc, h_inter, adjacency, Wd, eps, alpha,
         quantise_adjacency(8)
         mix(5)
         turn_g(0)
-        multiply((6, 7, 8), 0)
+        multiply((6, 7, 8), 2)
         keep_warm(early[:], 2)
         mix(6)
         mix(7)

from contextlib import ExitStack

import concourse.mybir as mybir
from concourse.masks import make_identity

BF16 = mybir.dt.bfloat16
F32 = mybir.dt.float32
U32 = mybir.dt.uint32
U8 = mybir.dt.uint8
FP8X4 = mybir.dt.float8_e4m3fn_x4
MULT = mybir.AluOpType.mult
ADD = mybir.AluOpType.add
COPY = mybir.ActivationFunctionType.Copy

P = 128
PACK = 4
S = 512
H = 4
HD = 128
D = 128
C = 4
PAIRED = H + 2
PIECES = [[(k % H, 2 * (k // H)), (k % H, 2 * (k // H) + 1)] for k in range(PAIRED)] + [
    [(2, 2), (3, 2)],
    [(2, 3)],
    [(3, 3)],
]
RUN = 4
WARM_COLUMNS = 256
WARM_PASSES = 13

TWO_ONES = 0x3F803F80

FLOPS = 2 * H * S * S * HD + 2 * S * (H * HD) * D


def regroup(engine_copy, grouped, rows):
    engine_copy(
        out=grouped.rearrange("p (x r) j -> p x j r", r=RUN),
        in_=rows.rearrange("p j (x r) -> p x j r", r=RUN),
    )


def tile_llamamlp_halfwaygin_pa_s_kernel(tc, h_inter, adjacency, Wd, eps, alpha, out):
    nc = tc.nc
    with ExitStack() as ctx:
        keep = ctx.enter_context(tc.tile_pool(name="keep", bufs=1))
        turned = ctx.enter_context(tc.psum_pool(name="turned", bufs=4))
        sums = ctx.enter_context(tc.psum_pool(name="sums", bufs=2))
        last = ctx.enter_context(tc.psum_pool(name="last", bufs=2))
        ctx.enter_context(tc.manual_schedule())

        h_sb = keep.tile([P, C, H * HD], BF16)
        nc.sync.dma_start(
            out=h_sb[:].rearrange("p (u e) i -> p u (e i)", u=2),
            in_=h_inter[0].rearrange("(u p e) i -> p u (e i)", u=2, e=2),
        )
        a_pairs = adjacency[0].rearrange("n (u p e) t -> u n p (e t)", u=2, e=2)
        a_rows = adjacency[0].rearrange("n (u p e) t -> u e p n t", u=2, e=2)
        a_sb = []
        eps_bc = keep.tile([P, H], BF16)
        alpha_bc = keep.tile([P, H], BF16)
        for x, blocks in enumerate(PIECES):
            n, c = blocks[0]
            a_piece = keep.tile([P, len(blocks), S], BF16, name="a_piece%d" % x)
            if x < PAIRED:
                nc.sync.dma_start(out=a_piece[:].rearrange("p e t -> p (e t)"), in_=a_pairs[c // 2, n])
            else:
                nc.sync.dma_start(out=a_piece[:], in_=a_rows[c // 2, c % 2][:, n : n + len(blocks), :])
            a_sb.append(a_piece)
            if x == 0:
                nc.scalar.dma_start(out=eps_bc[:], in_=eps.partition_broadcast(P))
                nc.scalar.dma_start(out=alpha_bc[:], in_=alpha.partition_broadcast(P))
        wd_sb = keep.tile([P, PACK, D], BF16)
        nc.sync.dma_start(
            out=wd_sb[:].rearrange("p (u e) j -> p u (e j)", u=2),
            in_=Wd.rearrange("(u p e) j -> p u (e j)", u=2, e=2),
        )

        zero = keep.tile([P, 1], F32)
        nc.vector.memset(zero[:], 0.0)
        unread_column = keep.tile([P, 1], F32)
        nc.scalar.activation(out=unread_column[:], in_=zero[:], func=COPY)

        ident = keep.tile([P, P], F32)
        make_identity(nc, ident[:])

        idle = keep.tile([P, WARM_COLUMNS * PACK], BF16, align_bytes=64)
        nc.vector.memset(idle[:].bitcast(U32), TWO_ONES)
        idle_codes = keep.tile([P, WARM_COLUMNS], U32, align_bytes=64)
        idle_scales = keep.tile([P, WARM_COLUMNS], U8, align_bytes=64)
        nc.vector.quantize_mx(out=idle_codes[:].bitcast(FP8X4), scales=idle_scales[:], in_=idle[:])

        def keep_warm(unread, passes):
            for warm_pass in range(passes):
                nc.tensor.matmul_mx(
                    out=unread,
                    lhsT=idle_codes[:, 0:P].bitcast(FP8X4),
                    lhsT_scale=idle_scales[:, 0:P],
                    rhs=idle_codes[:].bitcast(FP8X4),
                    rhs_scale=idle_scales[:],
                    start=True,
                    stop=True,
                )

        early = last.tile([P, WARM_COLUMNS], F32, tag="out_ps")
        keep_warm(early[:], WARM_PASSES)

        one_plus_eps = keep.tile([P, H], F32)
        nc.vector.tensor_scalar_add(out=one_plus_eps[:], in0=eps_bc[:], scalar1=1.0)
        h_term = keep.tile([P, C, H * HD], F32)

        def scale_h(n):
            cols = slice(n * HD, (n + 1) * HD)
            if n < H - 1:
                nc.scalar.activation(
                    out=h_term[:, :, cols], in_=h_sb[:, :, cols], func=COPY, scale=one_plus_eps[:, n : n + 1]
                )
            else:
                nc.vector.tensor_scalar_mul(
                    out=h_term[:, :, cols], in0=h_sb[:, :, cols], scalar1=one_plus_eps[:, n : n + 1]
                )

        h_grouped = keep.tile([P, H * HD, PACK], BF16, align_bytes=64)
        h_codes = keep.tile([P, H * HD], U32, align_bytes=64)
        h_scales = keep.tile([P, H * HD], U8, align_bytes=64)

        def quantise_h():
            halves = [slice(0, H * HD // 2), slice(H * HD // 2, H * HD)]
            for cols in halves:
                regroup(nc.vector.tensor_copy, h_grouped[:, cols, :], h_sb[:, :, cols])
            for cols in halves:
                nc.vector.quantize_mx(
                    out=h_codes[:, cols].bitcast(FP8X4),
                    scales=h_scales[:, cols],
                    in_=h_grouped[:, cols, :].rearrange("p i c -> p (i c)"),
                )

        wd_grouped = keep.tile([P, D, PACK], BF16, align_bytes=64)
        wd_codes = keep.tile([P, D], U32, align_bytes=64)
        wd_scales = keep.tile([P, D], U8, align_bytes=64)

        def regroup_wd():
            regroup(nc.scalar.copy, wd_grouped[:], wd_sb[:])

        def quantise_wd():
            nc.vector.quantize_mx(
                out=wd_codes[:].bitcast(FP8X4),
                scales=wd_scales[:],
                in_=wd_grouped[:].rearrange("p j k -> p (j k)"),
            )

        a_grouped = {}
        a_codes = {}
        a_scales = {}
        agg = {}
        g_sb = [keep.tile([P, 2, H * HD], BF16, align_bytes=64, name="g_sb%d" % u) for u in range(2)]

        def turn_adjacency(x):
            count = len(PIECES[x])
            a_turned = turned.tile([P, count, 2, P], F32, tag="turned")
            for r in range(count):
                row_words = a_sb[x][:, r, :].bitcast(F32)
                for u in range(2):
                    nc.tensor.transpose(a_turned[:, r, u, :], row_words[:, u * P : (u + 1) * P], ident[:])
            a_grouped[x] = keep.tile([P, count, P, PACK], BF16, align_bytes=64, name="a_grouped%d" % x)
            nc.scalar.copy(
                out=a_grouped[x][:]
                .rearrange("p r s k -> p (r s k)")
                .bitcast(F32)
                .rearrange("p (r s u) -> p r s u", r=count, u=2),
                in_=a_turned[:].rearrange("p r u s -> p r s u"),
            )

        def quantise_adjacency(x):
            count = len(PIECES[x])
            a_codes[x] = keep.tile([P, count * P], U32, align_bytes=64, name="a_codes%d" % x)
            a_scales[x] = keep.tile([P, count * P], U8, align_bytes=64, name="a_scales%d" % x)
            nc.vector.quantize_mx(
                out=a_codes[x][:].bitcast(FP8X4),
                scales=a_scales[x][:],
                in_=a_grouped[x][:].rearrange("p r s k -> p (r s k)"),
            )

        def multiply(pieces, warm_passes):
            bank = sums.tile([P, 4, HD], F32, name="bank", tag="bank")
            keep_warm(bank[:, 0:2, :].rearrange("p r d -> p (r d)"), warm_passes)
            place = 0
            for x in pieces:
                agg[x] = bank[:, place : place + len(PIECES[x]), :]
                for r, (n, c) in enumerate(PIECES[x]):
                    nc.tensor.matmul_mx(
                        out=bank[:, place, :],
                        lhsT=a_codes[x][:, r * P : (r + 1) * P].bitcast(FP8X4),
                        lhsT_scale=a_scales[x][:, r * P : (r + 1) * P],
                        rhs=h_codes[:, n * HD : (n + 1) * HD].bitcast(FP8X4),
                        rhs_scale=h_scales[:, n * HD : (n + 1) * HD],
                        start=True,
                        stop=True,
                    )
                    place += 1

        def mix(x):
            n, c = PIECES[x][0]
            if x < PAIRED:
                cols = slice(n * HD, (n + 1) * HD)
                parts = [(n, g_sb[c // 2][:, :, cols], agg[x], h_term[:, c : c + 2, cols])]
            else:
                parts = []
                for r in range(len(PIECES[x])):
                    cols = slice((n + r) * HD, (n + r + 1) * HD)
                    parts.append((n + r, g_sb[c // 2][:, c % 2, cols], agg[x][:, r, :], h_term[:, c, cols]))
            for head, g_part, agg_part, h_part in parts:
                nc.vector.scalar_tensor_tensor(
                    out=g_part, in0=agg_part, scalar=alpha_bc[:, head : head + 1], in1=h_part, op0=MULT, op1=ADD
                )

        g_grouped = {}
        g_codes = {}
        g_scales = {}
        out_sb = keep.tile([P, C, D], F32)
        out_rows = out[0].rearrange("(u p e) j -> u p e j", u=2, e=2)

        def slices_of(c):
            return 2 if c == 0 else 1

        def turn_g(c):
            count = slices_of(c)
            g_turned = turned.tile([P, count, 2, P], F32, tag="turned")
            for r in range(count):
                row_words = g_sb[c // 2][:, c % 2 + r, :].bitcast(F32)
                for u in range(2):
                    nc.tensor.transpose(g_turned[:, r, u, :], row_words[:, u * P : (u + 1) * P], ident[:])
            g_grouped[c] = keep.tile([P, count, P, PACK], BF16, align_bytes=64, name="g_grouped%d" % c)
            nc.scalar.copy(
                out=g_grouped[c][:]
                .rearrange("p r s k -> p (r s k)")
                .bitcast(F32)
                .rearrange("p (r s u) -> p r s u", r=count, u=2),
                in_=g_turned[:].rearrange("p r u s -> p r s u"),
            )

        def quantise_g(c):
            count = slices_of(c)
            g_codes[c] = keep.tile([P, count * P], U32, align_bytes=64, name="g_codes%d" % c)
            g_scales[c] = keep.tile([P, count * P], U8, align_bytes=64, name="g_scales%d" % c)
            nc.vector.quantize_mx(
                out=g_codes[c][:].bitcast(FP8X4),
                scales=g_scales[c][:],
                in_=g_grouped[c][:].rearrange("p r s k -> p (r s k)"),
            )

        def project(c):
            count = slices_of(c)
            out_ps = last.tile([P, count, D], F32, tag="out_ps")
            for r in range(count):
                nc.tensor.matmul_mx(
                    out=out_ps[:, r, :],
                    lhsT=g_codes[c][:, r * P : (r + 1) * P].bitcast(FP8X4),
                    lhsT_scale=g_scales[c][:, r * P : (r + 1) * P],
                    rhs=wd_codes[:].bitcast(FP8X4),
                    rhs_scale=wd_scales[:],
                    start=True,
                    stop=True,
                )
            nc.scalar.copy(out=out_sb[:, c : c + count, :], in_=out_ps[:])
            u, e = divmod(c, 2)
            nc.sync.dma_start(out=out_rows[u][:, e : e + count, :], in_=out_sb[:, c : c + count, :])

        scale_h(0)
        scale_h(1)
        scale_h(2)
        quantise_h()
        turn_adjacency(0)
        turn_adjacency(1)
        keep_warm(early[:], 4)
        turn_adjacency(2)
        quantise_adjacency(0)
        quantise_adjacency(1)
        scale_h(3)
        turn_adjacency(3)
        turn_adjacency(4)
        quantise_adjacency(2)
        quantise_adjacency(3)
        multiply((0, 1), 2)
        mix(0)
        mix(1)
        turn_adjacency(5)
        turn_adjacency(6)
        quantise_adjacency(4)
        quantise_adjacency(5)
        multiply((2, 3), 1)
        mix(2)
        mix(3)
        turn_adjacency(7)
        turn_adjacency(8)
        regroup_wd()
        quantise_adjacency(6)
        quantise_adjacency(7)
        multiply((4, 5), 2)
        mix(4)
        quantise_adjacency(8)
        mix(5)
        turn_g(0)
        multiply((6, 7, 8), 2)
        keep_warm(early[:], 2)
        mix(6)
        mix(7)
        mix(8)
        turn_g(2)
        turn_g(3)
        quantise_g(0)
        quantise_wd()
        quantise_g(2)
        quantise_g(3)
        project(0)
        project(2)
        project(3)
